import numpy as np
import ml_dtypes


def mxq(x, axis, fmt="e4m3"):
    dtype, down = {"e4m3": (ml_dtypes.float8_e4m3fn, 7), "e5m2": (ml_dtypes.float8_e5m2, 14)}[fmt]
    v = np.moveaxis(np.asarray(x, np.float32).astype(ml_dtypes.bfloat16).astype(np.float64), axis, -1)
    blocks = v.reshape(v.shape[:-1] + (-1, 32))
    amax = np.abs(blocks).max(-1, keepdims=True)
    byte = np.maximum(np.where(amax > 0, np.frexp(amax)[1] - 1 + 127, 0) - down, 1)
    scale = np.exp2(byte - 127.0)
    codes = (blocks / scale).astype(np.float32).astype(dtype).astype(np.float64)
    return np.moveaxis((codes * scale).reshape(v.shape), -1, axis)


WIDE = False


def mx_kscale(k):
    if not WIDE:
        return np.ones(k)
    levels = np.array([10, -10, 5, -5, 0])
    a = np.random.permutation(np.resize(levels, k // 512 * 4)).reshape(k // 512, 4)
    idx = np.arange(k)
    return np.exp2(a[idx // 512, idx % 128 // 32])


BF16 = ml_dtypes.bfloat16


def bf(x):
    return np.asarray(x, np.float32).astype(BF16)


def f64(x):
    return np.asarray(x).astype(np.float64)


B, D, H, G, L, P = 256, 1024, 1024, 4, 4, 2


def sigmoid(v):
    return 1.0 / (1.0 + np.exp(-v))


def setup_inputs():
    s, u = mx_kscale(H), mx_kscale(H)
    w_ih = np.random.standard_normal((G, P, H, H)) * 1.5 / np.sqrt(H)
    w_ih[:, 0] = w_ih[:, 0] / s[:, None]
    w_hh = np.random.standard_normal((G, P, H, H)) / np.sqrt(H) / u[:, None]
    return {"x": bf(np.random.standard_normal((B, H)) * s),
            "hidden": bf(np.random.standard_normal((B, H)) * u),
            "cell_state": bf(np.random.standard_normal((B, H))),
            "w_ih": bf(w_ih),
            "w_hh": bf(w_hh),
            "b_ih": bf(np.random.standard_normal((G, P, H)) * 0.3),
            "b_hh": bf(np.random.standard_normal((G, P, H)) * 0.3)}


def reference(x, hidden, cell_state, w_ih, w_hh, b_ih, b_hh):
    x, c = f64(x), f64(cell_state)
    w_ih, w_hh, b_ih, b_hh = f64(w_ih), f64(w_hh), f64(b_ih), f64(b_hh)
    hq = mxq(f64(hidden), 1, "e4m3")
    for l in range(P):
        gates = ((mxq(x, 1, "e4m3") @ mxq(w_ih[:, l], 1, "e4m3"))
                 + (hq @ mxq(w_hh[:, l], 1, "e4m3"))
                 + b_ih[:, l][:, None, :] + b_hh[:, l][:, None, :])
        z_i, z_f, z_g, z_o = gates
        i_t = sigmoid(z_i)
        f_t = sigmoid(z_f)
        g_t = np.tanh(z_g)
        o_t = sigmoid(z_o)
        c = f_t * c + i_t * g_t
        x = o_t * np.tanh(c)
    return x, c

@@ -1,0 +1,273 @@
+from contextlib import ExitStack
+
+import concourse.mybir as mybir
+from concourse.masks import make_identity
+
+BF16 = mybir.dt.bfloat16
+F32 = mybir.dt.float32
+U32 = mybir.dt.uint32
+U8 = mybir.dt.uint8
+FP8X4 = mybir.dt.float8_e4m3fn_x4
+SIGMOID = mybir.ActivationFunctionType.Sigmoid
+TANH = mybir.ActivationFunctionType.Tanh
+
+P = 128
+PACK = 4
+K_PASS = P * PACK
+B = 256
+H = 1024
+LAYERS = 2
+PASSES = H // K_PASS
+HALF = H // 2
+TILES = HALF // P
+B_TILES = B // P
+
+GATE_ORDER = (0, 2, 1, 3)
+CHUNKS_PER_GATE = 2 * PASSES
+N_GATES = len(GATE_ORDER)
+N_CHUNKS = LAYERS * N_GATES * CHUNKS_PER_GATE
+N_STEPS = 2 * N_CHUNKS
+RAW_BUFS = 2 * CHUNKS_PER_GATE
+VECTOR_COLS = 256
+
+FLOPS = 2 * LAYERS * N_GATES * 2 * B * H * H
+
+
+def tile_lstm_pa_kernel(tc, x, hidden, cell_state, w_ih, w_hh, b_ih, b_hh, out_0, out_1):
+    nc = tc.nc
+    with ExitStack() as ctx:
+        const = ctx.enter_context(tc.tile_pool(name="const", bufs=1))
+        rows_pool = ctx.enter_context(tc.tile_pool(name="rows", bufs=1))
+        raw_pool = ctx.enter_context(tc.tile_pool(name="raw", bufs=RAW_BUFS))
+        grouped_pool = ctx.enter_context(tc.tile_pool(name="grouped", bufs=4))
+        codes_pool = ctx.enter_context(tc.tile_pool(name="codes", bufs=6))
+        gate_pool = ctx.enter_context(tc.tile_pool(name="gate", bufs=2))
+        cell_pool = ctx.enter_context(tc.tile_pool(name="cell", bufs=4))
+        store_pool = ctx.enter_context(tc.tile_pool(name="store", bufs=4))
+        z_pool = ctx.enter_context(tc.psum_pool(name="z", bufs=6))
+        flip_pool = ctx.enter_context(tc.psum_pool(name="flip", bufs=2))
+
+        def load_rows(src, name):
+            rows = rows_pool.tile([P, B_TILES, H], BF16, name=name)
+            nc.sync.dma_start(out=rows[:], in_=src.rearrange("(a p) k -> p a k", p=P))
+            return rows
+
+        hidden_rows = load_rows(hidden, "hidden_rows")
+        x_rows = load_rows(x, "x_rows")
+        bias_rows = const.tile([P, P], BF16)
+        half_p = P // 2
+        nc.sync.dma_start(out=bias_rows[0:half_p, :], in_=b_ih.rearrange("k l (j p) -> (k l j) p", p=P))
+        nc.sync.dma_start(out=bias_rows[half_p:P, :], in_=b_hh.rearrange("k l (j p) -> (k l j) p", p=P))
+        cell_rows = load_rows(cell_state, "cell_rows")
+
+        raw = {}
+
+        def load_chunk(c):
+            layer, pos, q = c // (N_GATES * CHUNKS_PER_GATE), (c // CHUNKS_PER_GATE) % N_GATES, c % CHUNKS_PER_GATE
+            w = w_hh if q < PASSES else w_ih
+            g = q % PASSES
+            k_rows = w[GATE_ORDER[pos], layer, g * K_PASS : (g + 1) * K_PASS, :]
+            if layer == 1 and q >= PASSES:
+                view = k_rows.rearrange("(t p) n -> p t n", p=P)
+            else:
+                view = k_rows.rearrange("(p t) n -> p t n", t=PACK)
+            raw[c] = raw_pool.tile([P, PACK, H], BF16, name="raw")
+            nc.sync.dma_start(out=raw[c][:], in_=view)
+
+        for c in range(RAW_BUFS):
+            load_chunk(c)
+
+        ident_f32 = const.tile([P, P], F32)
+        make_identity(nc, ident_f32[:])
+        ident_bf16 = const.tile([P, P], BF16)
+        make_identity(nc, ident_bf16[:])
+        warm = const.tile([P, 1], F32)
+        nc.vector.memset(warm[:], 0.0)
+        nc.scalar.activation(out=warm[:], in_=warm[:], func=SIGMOID)
+
+        def quantise_rows(rows, name):
+            words = rows[:].bitcast(F32)
+            grouped = rows_pool.tile([P, PASSES, B * PACK], BF16, name=name + "_grouped", align_bytes=64)
+            grouped_words = grouped[:].bitcast(F32)
+            for g in range(PASSES):
+                flipped = flip_pool.tile([P, 2, B], F32, name="flipped", tag="flip")
+                for u in range(2):
+                    for a in range(B_TILES):
+                        first = g * (K_PASS // 2) + u
+                        nc.tensor.transpose(
+                            flipped[:, u, a * P : (a + 1) * P],
+                            words[:, a, first : (g + 1) * (K_PASS // 2) : 2],
+                            ident_f32[:],
+                        )
+                dst = grouped_words[:, g, :].rearrange("p (b u) -> p b u", u=2)
+                src = flipped[:].rearrange("p u b -> p b u")
+                if g == 0:
+                    nc.vector.tensor_copy(out=dst, in_=src)
+                else:
+                    nc.scalar.copy(out=dst, in_=src)
+            return grouped
+
+        def quantise_moving(grouped, name):
+            codes = const.tile([P, PASSES, B], U32, name=name + "_codes", align_bytes=64)
+            scales = const.tile([P, PASSES, B], U8, name=name + "_scales", align_bytes=64)
+            nc.vector.quantize_mx(
+                out=codes[:].rearrange("p g b -> p (g b)").bitcast(FP8X4),
+                scales=scales[:].rearrange("p g b -> p (g b)"),
+                in_=grouped[:].rearrange("p g c -> p (g c)"),
+            )
+            return codes, scales
+
+        hidden_grouped = quantise_rows(hidden_rows, "hidden")
+        x_grouped = quantise_rows(x_rows, "x")
+        hidden_mx = quantise_moving(hidden_grouped, "hidden")
+        x_mx = {0: quantise_moving(x_grouped, "x")}
+
+        bias_flipped = flip_pool.tile([P, P], BF16, name="bias_flipped", tag="flip")
+        nc.tensor.transpose(bias_flipped[:], bias_rows[:], ident_bf16[:])
+        bias_both = const.tile([P, P], F32)
+        nc.vector.tensor_copy(out=bias_both[:], in_=bias_flipped[:])
+        bias = const.tile([P, half_p], F32)
+        nc.vector.tensor_add(out=bias[:], in0=bias_both[:, 0:half_p], in1=bias_both[:, half_p:P])
+
+        cell = {}
+        for hf in range(2):
+            cell_flipped = flip_pool.tile([P, TILES, B], BF16, name="cell_flipped", tag="flip")
+            for jt in range(TILES):
+                for a in range(B_TILES):
+                    first = hf * HALF + jt * P
+                    nc.tensor.transpose(
+                        cell_flipped[:, jt, a * P : (a + 1) * P], cell_rows[:, a, first : first + P], ident_bf16[:]
+                    )
+            cell[(0, hf)] = cell_pool.tile([P, TILES, B], F32, name="cell")
+            if hf == 0:
+                nc.vector.tensor_copy(out=cell[(0, hf)][:], in_=cell_flipped[:])
+            else:
+                nc.scalar.copy(out=cell[(0, hf)][:], in_=cell_flipped[:])
+
+        grouped = {}
+        z = {}
+        gate_sb = {}
+        tanh_c = {}
+        flipped_out = {}
+        x1_grouped = rows_pool.tile([P, PASSES, B * PACK], BF16, align_bytes=64)
+
+        def unit_of(u):
+            return u // (2 * N_GATES), (u // 2) % N_GATES, u % 2
+
+        def regroup(s):
+            u, q = s // CHUNKS_PER_GATE, s % CHUNKS_PER_GATE
+            layer, pos, hf = unit_of(u)
+            c = (layer * N_GATES + pos) * CHUNKS_PER_GATE + q
+            grouped[s] = grouped_pool.tile([P, HALF, PACK], BF16, name="grouped", align_bytes=64)
+            first = hf * HALF
+            split = first + VECTOR_COLS
+            nc.vector.tensor_copy(
+                out=grouped[s][:, 0:VECTOR_COLS, :].rearrange("p (c i) t -> p c t i", i=4),
+                in_=raw[c][:, :, first:split].rearrange("p t (c i) -> p c t i", i=4),
+            )
+            nc.scalar.copy(
+                out=grouped[s][:, VECTOR_COLS:HALF, :].rearrange("p (c i) t -> p c t i", i=4),
+                in_=raw[c][:, :, split : first + HALF].rearrange("p t (c i) -> p c t i", i=4),
+            )
+            if hf == 1 and c + RAW_BUFS < N_CHUNKS:
+                load_chunk(c + RAW_BUFS)
+
+        def quantise_and_multiply(s):
+            u, q = s // CHUNKS_PER_GATE, s % CHUNKS_PER_GATE
+            layer, pos, hf = unit_of(u)
+            codes = codes_pool.tile([P, HALF], U32, name="codes", align_bytes=64)
+            scales = codes_pool.tile([P, HALF], U8, name="scales", align_bytes=64)
+            nc.vector.quantize_mx(
+                out=codes[:].bitcast(FP8X4), scales=scales[:], in_=grouped[s][:].rearrange("p n t -> p (n t)")
+            )
+            if q == 0:
+                z[u] = [z_pool.tile([P, B], F32, name="z", tag="z") for jt in range(TILES)]
+            moving_codes, moving_scales = hidden_mx if q < PASSES else x_mx[layer]
+            g = q % PASSES
+            for jt in range(TILES):
+                nc.tensor.matmul_mx(
+                    out=z[u][jt][:],
+                    lhsT=codes[:, jt * P : (jt + 1) * P].bitcast(FP8X4),
+                    lhsT_scale=scales[:, jt * P : (jt + 1) * P],
+                    rhs=moving_codes[:, g, :].bitcast(FP8X4),
+                    rhs_scale=moving_scales[:, g, :],
+                    start=(q == 0),
+                    stop=(q == CHUNKS_PER_GATE - 1),
+                )
+
+        def activate(u):
+            layer, pos, hf = unit_of(u)
+            gate = GATE_ORDER[pos]
+            gate_sb[u] = gate_pool.tile([P, TILES, B], F32, name="gate%d" % gate)
+            for jt in range(TILES):
+                col = (gate * LAYERS + layer) * (H // P) + hf * TILES + jt
+                nc.scalar.activation(
+                    out=gate_sb[u][:, jt, :],
+                    in_=z[u][jt][:],
+                    func=(TANH if gate == 2 else SIGMOID),
+                    bias=bias[:, col : col + 1],
+                    scale=1.0,
+                )
+
+        def flip_out(src, key):
+            flipped_out[key] = []
+            for a in range(B_TILES):
+                flipped = flip_pool.tile([P, HALF], F32, name="flipped_out", tag="flip")
+                for jt in range(TILES):
+                    nc.tensor.transpose(flipped[:, jt * P : (jt + 1) * P], src[:, jt, a * P : (a + 1) * P], ident_f32[:])
+                flipped_out[key].append(flipped)
+
+        def store(key, out, hf):
+            for a in range(B_TILES):
+                rows = store_pool.tile([P, HALF], F32, name="out_rows")
+                if a == 0:
+                    nc.vector.tensor_copy(out=rows[:], in_=flipped_out[key][a][:])
+                else:
+                    nc.scalar.copy(out=rows[:], in_=flipped_out[key][a][:])
+                nc.sync.dma_start(out=out[a * P : (a + 1) * P, hf * HALF : (hf + 1) * HALF], in_=rows[:])
+
+        def update_cell(u):
+            layer, pos, hf = unit_of(u)
+            if pos == 1:
+                nc.vector.tensor_mul(out=gate_sb[u - 2][:], in0=gate_sb[u - 2][:], in1=gate_sb[u][:])
+            if pos == 2:
+                nc.vector.tensor_mul(out=gate_sb[u][:], in0=gate_sb[u][:], in1=cell[(layer, hf)][:])
+                cell[(layer + 1, hf)] = cell_pool.tile([P, TILES, B], F32, name="cell")
+                nc.vector.tensor_add(out=cell[(layer + 1, hf)][:], in0=gate_sb[u][:], in1=gate_sb[u - 4][:])
+                if layer == LAYERS - 1:
+                    flip_out(cell[(layer + 1, hf)], u)
+            if pos == 3:
+                if layer == 0:
+                    nc.vector.tensor_mul(
+                        out=x1_grouped[:, hf, :].rearrange("p (b t) -> p b t", t=PACK),
+                        in0=gate_sb[u][:].rearrange("p t b -> p b t"),
+                        in1=tanh_c[(layer, hf)][:].rearrange("p t b -> p b t"),
+                    )
+                    if hf == 1:
+                        x_mx[1] = quantise_moving(x1_grouped, "x1")
+                else:
+                    nc.vector.tensor_mul(out=gate_sb[u][:], in0=gate_sb[u][:], in1=tanh_c[(layer, hf)][:])
+                    flip_out(gate_sb[u], u)
+
+        def after_cell(u):
+            layer, pos, hf = unit_of(u)
+            if pos == 2:
+                tanh_c[(layer, hf)] = gate_pool.tile([P, TILES, B], F32, name="tanh_c")
+                nc.scalar.activation(out=tanh_c[(layer, hf)][:], in_=cell[(layer + 1, hf)][:], func=TANH)
+                if layer == LAYERS - 1:
+                    store(u, out_1, hf)
+            if pos == 3 and layer == LAYERS - 1:
+                store(u, out_0, hf)
+
+        last = CHUNKS_PER_GATE - 1
+        for s in range(N_STEPS + 7):
+            if s < N_STEPS:
+                regroup(s)
+            if 2 <= s < N_STEPS + 2 and (s - 2) % CHUNKS_PER_GATE == last:
+                activate((s - 2) // CHUNKS_PER_GATE)
+            if 4 <= s < N_STEPS + 4 and (s - 4) % CHUNKS_PER_GATE == last:
+                update_cell((s - 4) // CHUNKS_PER_GATE)
+            if 6 <= s < N_STEPS + 6 and (s - 6) % CHUNKS_PER_GATE == last:
+                after_cell((s - 6) // CHUNKS_PER_GATE)
+            if 1 <= s <= N_STEPS:
+                quantise_and_multiply(s - 1)

@@ -42,7 +42,8 @@ def tile_lstm_pa_kernel(tc, x, hidden, cell_state, w_ih, w_hh, b_ih, b_hh, out_0
         grouped_pool = ctx.enter_context(tc.tile_pool(name="grouped", bufs=4))
         codes_pool = ctx.enter_context(tc.tile_pool(name="codes", bufs=6))
         gate_pool = ctx.enter_context(tc.tile_pool(name="gate", bufs=2))
-        cell_pool = ctx.enter_context(tc.tile_pool(name="cell", bufs=4))
+        cell_pool = ctx.enter_context(tc.tile_pool(name="cell", bufs=2))
+        tanh_pool = ctx.enter_context(tc.tile_pool(name="tanh", bufs=2 * B_TILES))
         store_pool = ctx.enter_context(tc.tile_pool(name="store", bufs=4))
         z_pool = ctx.enter_context(tc.psum_pool(name="z", bufs=6))
         flip_pool = ctx.enter_context(tc.psum_pool(name="flip", bufs=2))
@@ -138,7 +139,7 @@ def tile_lstm_pa_kernel(tc, x, hidden, cell_state, w_ih, w_hh, b_ih, b_hh, out_0
                     nc.tensor.transpose(
                         cell_flipped[:, jt, a * P : (a + 1) * P], cell_rows[:, a, first : first + P], ident_bf16[:]
                     )
-            cell[(0, hf)] = cell_pool.tile([P, TILES, B], F32, name="cell")
+            cell[(0, hf)] = const.tile([P, TILES, B], BF16, name="cell_0_%d" % hf)
             if hf == 0:
                 nc.vector.tensor_copy(out=cell[(0, hf)][:], in_=cell_flipped[:])
             else:
@@ -209,22 +210,24 @@ def tile_lstm_pa_kernel(tc, x, hidden, cell_state, w_ih, w_hh, b_ih, b_hh, out_0
                     scale=1.0,
                 )
 
-        def flip_out(src, key):
+        def flip_sum(terms, key):
             flipped_out[key] = []
             for a in range(B_TILES):
                 flipped = flip_pool.tile([P, HALF], F32, name="flipped_out", tag="flip")
                 for jt in range(TILES):
-                    nc.tensor.transpose(flipped[:, jt * P : (jt + 1) * P], src[:, jt, a * P : (a + 1) * P], ident_f32[:])
+                    for i, term in enumerate(terms):
+                        nc.tensor.matmul(
+                            flipped[:, jt * P : (jt + 1) * P],
+                            lhsT=term[:, jt, a * P : (a + 1) * P],
+                            rhs=ident_f32[:],
+                            is_transpose=True,
+                            start=(i == 0),
+                            stop=(i == len(terms) - 1),
+                        )
                 flipped_out[key].append(flipped)
 
-        def store(key, out, hf):
-            for a in range(B_TILES):
-                rows = store_pool.tile([P, HALF], F32, name="out_rows")
-                if a == 0:
-                    nc.vector.tensor_copy(out=rows[:], in_=flipped_out[key][a][:])
-                else:
-                    nc.scalar.copy(out=rows[:], in_=flipped_out[key][a][:])
-                nc.sync.dma_start(out=out[a * P : (a + 1) * P, hf * HALF : (hf + 1) * HALF], in_=rows[:])
+        def store_rows(rows, out, a, hf):
+            nc.sync.dma_start(out=out[a * P : (a + 1) * P, hf * HALF : (hf + 1) * HALF], in_=rows[:])
 
         def update_cell(u):
             layer, pos, hf = unit_of(u)
@@ -232,10 +235,11 @@ def tile_lstm_pa_kernel(tc, x, hidden, cell_state, w_ih, w_hh, b_ih, b_hh, out_0
                 nc.vector.tensor_mul(out=gate_sb[u - 2][:], in0=gate_sb[u - 2][:], in1=gate_sb[u][:])
             if pos == 2:
                 nc.vector.tensor_mul(out=gate_sb[u][:], in0=gate_sb[u][:], in1=cell[(layer, hf)][:])
-                cell[(layer + 1, hf)] = cell_pool.tile([P, TILES, B], F32, name="cell")
-                nc.vector.tensor_add(out=cell[(layer + 1, hf)][:], in0=gate_sb[u][:], in1=gate_sb[u - 4][:])
-                if layer == LAYERS - 1:
-                    flip_out(cell[(layer + 1, hf)], u)
+                if layer == 0:
+                    cell[(1, hf)] = cell_pool.tile([P, TILES, B], F32, name="cell")
+                    nc.vector.tensor_add(out=cell[(1, hf)][:], in0=gate_sb[u][:], in1=gate_sb[u - 4][:])
+                else:
+                    flip_sum((gate_sb[u], gate_sb[u - 4]), u)
             if pos == 3:
                 if layer == 0:
                     nc.vector.tensor_mul(
@@ -246,18 +250,26 @@ def tile_lstm_pa_kernel(tc, x, hidden, cell_state, w_ih, w_hh, b_ih, b_hh, out_0
                     if hf == 1:
                         x_mx[1] = quantise_moving(x1_grouped, "x1")
                 else:
-                    nc.vector.tensor_mul(out=gate_sb[u][:], in0=gate_sb[u][:], in1=tanh_c[(layer, hf)][:])
-                    flip_out(gate_sb[u], u)
+                    flip_sum((gate_sb[u],), u)
+                    for a in range(B_TILES):
+                        rows = store_pool.tile([P, HALF], F32, name="out_rows")
+                        nc.vector.tensor_mul(out=rows[:], in0=flipped_out[u][a][:], in1=tanh_c[(1, hf)][a][:])
+                        store_rows(rows, out_0, a, hf)
 
         def after_cell(u):
             layer, pos, hf = unit_of(u)
-            if pos == 2:
-                tanh_c[(layer, hf)] = gate_pool.tile([P, TILES, B], F32, name="tanh_c")
-                nc.scalar.activation(out=tanh_c[(layer, hf)][:], in_=cell[(layer + 1, hf)][:], func=TANH)
-                if layer == LAYERS - 1:
-                    store(u, out_1, hf)
-            if pos == 3 and layer == LAYERS - 1:
-                store(u, out_0, hf)
+            if pos == 2 and layer == 0:
+                tanh_c[(0, hf)] = gate_pool.tile([P, TILES, B], F32, name="tanh_c")
+                nc.scalar.activation(out=tanh_c[(0, hf)][:], in_=cell[(1, hf)][:], func=TANH)
+            if pos == 2 and layer == 1:
+                tanh_c[(1, hf)] = []
+                for a in range(B_TILES):
+                    rows = store_pool.tile([P, HALF], F32, name="out_rows")
+                    nc.scalar.copy(out=rows[:], in_=flipped_out[u][a][:])
+                    store_rows(rows, out_1, a, hf)
+                    tanh_rows = tanh_pool.tile([P, HALF], F32, name="tanh_rows")
+                    nc.scalar.activation(out=tanh_rows[:], in_=flipped_out[u][a][:], func=TANH)
+                    tanh_c[(1, hf)].append(tanh_rows)
 
         last = CHUNKS_PER_GATE - 1
         for s in range(N_STEPS + 7):

@@ -28,7 +28,7 @@ N_GATES = len(GATE_ORDER)
 N_CHUNKS = LAYERS * N_GATES * CHUNKS_PER_GATE
 N_STEPS = 2 * N_CHUNKS
 RAW_BUFS = 2 * CHUNKS_PER_GATE
-VECTOR_COLS = 256
+VECTOR_COLS = 272
 
 FLOPS = 2 * LAYERS * N_GATES * 2 * B * H * H
 
@@ -163,12 +163,12 @@ def tile_lstm_pa_kernel(tc, x, hidden, cell_state, w_ih, w_hh, b_ih, b_hh, out_0
             first = hf * HALF
             split = first + VECTOR_COLS
             nc.vector.tensor_copy(
-                out=grouped[s][:, 0:VECTOR_COLS, :].rearrange("p (c i) t -> p c t i", i=4),
-                in_=raw[c][:, :, first:split].rearrange("p t (c i) -> p c t i", i=4),
+                out=grouped[s][:, 0:VECTOR_COLS, :].rearrange("p (c i) t -> p c t i", i=2),
+                in_=raw[c][:, :, first:split].rearrange("p t (c i) -> p c t i", i=2),
             )
             nc.scalar.copy(
-                out=grouped[s][:, VECTOR_COLS:HALF, :].rearrange("p (c i) t -> p c t i", i=4),
-                in_=raw[c][:, :, split : first + HALF].rearrange("p t (c i) -> p c t i", i=4),
+                out=grouped[s][:, VECTOR_COLS:HALF, :].rearrange("p (c i) t -> p c t i", i=2),
+                in_=raw[c][:, :, split : first + HALF].rearrange("p t (c i) -> p c t i", i=2),
             )
             if hf == 1 and c + RAW_BUFS < N_CHUNKS:
                 load_chunk(c + RAW_BUFS)

@@ -23,14 +23,35 @@ TILES = HALF // P
 B_TILES = B // P
 
 GATE_ORDER = (0, 2, 1, 3)
-CHUNKS_PER_GATE = 2 * PASSES
 N_GATES = len(GATE_ORDER)
+CHUNKS_PER_GATE = 2 * PASSES
 N_CHUNKS = LAYERS * N_GATES * CHUNKS_PER_GATE
-N_STEPS = 2 * N_CHUNKS
-RAW_BUFS = 2 * CHUNKS_PER_GATE
-VECTOR_COLS = 272
+RAW_BUFS = 6
+TENSOR_SHARE = 1 / 5
+VECTOR_SHARE = 5 / 8
+TENSOR_LEAD = 4
+SCALAR_LEAD = 3
+QUANT_LAG = 1
+HEAD_SHARE = 17 / 32
+TAIL_SHARE = 7 / 8
+C2_ON_VECTOR = 0
+SHARED_HEAD = 4
+ACT_LAG = 1
+CELL_LAG = 3
+TANH_LAG = 5
+CODES_BUFS = 6
+Z_BUFS = 6
+
+
+MIX_COLS = 256
 
 FLOPS = 2 * LAYERS * N_GATES * 2 * B * H * H
+
+
+def list_units():
+    units = [(layer, pos, hf * HALF, HALF) for layer in range(LAYERS) for pos in range(N_GATES) for hf in range(2)]
+    quarter = HALF // 2
+    return units[:-1] + [(LAYERS - 1, N_GATES - 1, HALF + i * quarter, quarter) for i in range(2)]
 
 
 def tile_lstm_pa_kernel(tc, x, hidden, cell_state, w_ih, w_hh, b_ih, b_hh, out_0, out_1):
@@ -38,44 +59,60 @@ def tile_lstm_pa_kernel(tc, x, hidden, cell_state, w_ih, w_hh, b_ih, b_hh, out_0
     with ExitStack() as ctx:
         const = ctx.enter_context(tc.tile_pool(name="const", bufs=1))
         rows_pool = ctx.enter_context(tc.tile_pool(name="rows", bufs=1))
+        raw_half_pool = ctx.enter_context(tc.tile_pool(name="raw_half", bufs=2 * CHUNKS_PER_GATE))
         raw_pool = ctx.enter_context(tc.tile_pool(name="raw", bufs=RAW_BUFS))
-        grouped_pool = ctx.enter_context(tc.tile_pool(name="grouped", bufs=4))
-        codes_pool = ctx.enter_context(tc.tile_pool(name="codes", bufs=6))
+        grouped_pool = ctx.enter_context(tc.tile_pool(name="grouped", bufs=SCALAR_LEAD + QUANT_LAG + 2))
+        codes_pool = ctx.enter_context(tc.tile_pool(name="codes", bufs=CODES_BUFS))
         gate_pool = ctx.enter_context(tc.tile_pool(name="gate", bufs=2))
         cell_pool = ctx.enter_context(tc.tile_pool(name="cell", bufs=2))
         tanh_pool = ctx.enter_context(tc.tile_pool(name="tanh", bufs=2 * B_TILES))
-        store_pool = ctx.enter_context(tc.tile_pool(name="store", bufs=4))
-        z_pool = ctx.enter_context(tc.psum_pool(name="z", bufs=6))
-        flip_pool = ctx.enter_context(tc.psum_pool(name="flip", bufs=2))
+        store_pool = ctx.enter_context(tc.tile_pool(name="store", bufs=8))
+        z_pool = ctx.enter_context(tc.psum_pool(name="z", bufs=Z_BUFS))
+        flip_pool = ctx.enter_context(tc.psum_pool(name="flip", bufs=8 - Z_BUFS))
 
         def load_rows(src, name):
             rows = rows_pool.tile([P, B_TILES, H], BF16, name=name)
             nc.sync.dma_start(out=rows[:], in_=src.rearrange("(a p) k -> p a k", p=P))
             return rows
 
-        hidden_rows = load_rows(hidden, "hidden_rows")
-        x_rows = load_rows(x, "x_rows")
-        bias_rows = const.tile([P, P], BF16)
-        half_p = P // 2
-        nc.sync.dma_start(out=bias_rows[0:half_p, :], in_=b_ih.rearrange("k l (j p) -> (k l j) p", p=P))
-        nc.sync.dma_start(out=bias_rows[half_p:P, :], in_=b_hh.rearrange("k l (j p) -> (k l j) p", p=P))
-        cell_rows = load_rows(cell_state, "cell_rows")
-
         raw = {}
 
-        def load_chunk(c):
+        def chunk_view(c):
             layer, pos, q = c // (N_GATES * CHUNKS_PER_GATE), (c // CHUNKS_PER_GATE) % N_GATES, c % CHUNKS_PER_GATE
             w = w_hh if q < PASSES else w_ih
             g = q % PASSES
             k_rows = w[GATE_ORDER[pos], layer, g * K_PASS : (g + 1) * K_PASS, :]
             if layer == 1 and q >= PASSES:
-                view = k_rows.rearrange("(t p) n -> p t n", p=P)
-            else:
-                view = k_rows.rearrange("(p t) n -> p t n", t=PACK)
-            raw[c] = raw_pool.tile([P, PACK, H], BF16, name="raw")
-            nc.sync.dma_start(out=raw[c][:], in_=view)
+                return k_rows.rearrange("(t p) n -> p t n", p=P)
+            return k_rows.rearrange("(p t) n -> p t n", t=PACK)
 
-        for c in range(RAW_BUFS):
+        def load_half(c, hf):
+            tile = raw_half_pool.tile([P, PACK, HALF], BF16, name="raw_half")
+            nc.sync.dma_start(out=tile[:], in_=chunk_view(c)[:, :, hf * HALF : (hf + 1) * HALF])
+            raw[(c, hf)] = tile[:]
+
+        def load_chunk(c):
+            tile = raw_pool.tile([P, PACK, H], BF16, name="raw")
+            nc.sync.dma_start(out=tile[:], in_=chunk_view(c))
+            for hf in range(2):
+                raw[(c, hf)] = tile[:, :, hf * HALF : (hf + 1) * HALF]
+
+        half_p = P // 2
+        bias_rows = const.tile([P, P], BF16)
+        nc.scalar.dma_start(out=bias_rows[0:half_p, :], in_=b_ih.rearrange("k l (j p) -> (k l j) p", p=P))
+        nc.scalar.dma_start(out=bias_rows[half_p:P, :], in_=b_hh.rearrange("k l (j p) -> (k l j) p", p=P))
+
+        load_half(0, 0)
+        hidden_rows = load_rows(hidden, "hidden_rows")
+        load_half(1, 0)
+        x_rows = load_rows(x, "x_rows")
+        load_half(2, 0)
+        load_half(3, 0)
+        for c in range(CHUNKS_PER_GATE):
+            load_half(c, 1)
+        load_chunk(CHUNKS_PER_GATE)
+        cell_rows = load_rows(cell_state, "cell_rows")
+        for c in range(CHUNKS_PER_GATE + 1, CHUNKS_PER_GATE + RAW_BUFS):
             load_chunk(c)
 
         ident_f32 = const.tile([P, P], F32)
@@ -85,6 +122,16 @@ def tile_lstm_pa_kernel(tc, x, hidden, cell_state, w_ih, w_hh, b_ih, b_hh, out_0
         warm = const.tile([P, 1], F32)
         nc.vector.memset(warm[:], 0.0)
         nc.scalar.activation(out=warm[:], in_=warm[:], func=SIGMOID)
+
+        def quantise_moving(grouped, name):
+            codes = const.tile([P, PASSES, B], U32, name=name + "_codes", align_bytes=64)
+            scales = const.tile([P, PASSES, B], U8, name=name + "_scales", align_bytes=64)
+            nc.vector.quantize_mx(
+                out=codes[:].rearrange("p g b -> p (g b)").bitcast(FP8X4),
+                scales=scales[:].rearrange("p g b -> p (g b)"),
+                in_=grouped[:].rearrange("p g c -> p (g c)"),
+            )
+            return codes, scales
 
         def quantise_rows(rows, name):
             words = rows[:].bitcast(F32)
@@ -106,32 +153,20 @@ def tile_lstm_pa_kernel(tc, x, hidden, cell_state, w_ih, w_hh, b_ih, b_hh, out_0
                     nc.vector.tensor_copy(out=dst, in_=src)
                 else:
                     nc.scalar.copy(out=dst, in_=src)
-            return grouped
+            return quantise_moving(grouped, name)
 
-        def quantise_moving(grouped, name):
-            codes = const.tile([P, PASSES, B], U32, name=name + "_codes", align_bytes=64)
-            scales = const.tile([P, PASSES, B], U8, name=name + "_scales", align_bytes=64)
-            nc.vector.quantize_mx(
-                out=codes[:].rearrange("p g b -> p (g b)").bitcast(FP8X4),
-                scales=scales[:].rearrange("p g b -> p (g b)"),
-                in_=grouped[:].rearrange("p g c -> p (g c)"),
-            )
-            return codes, scales
-
-        hidden_grouped = quantise_rows(hidden_rows, "hidden")
-        x_grouped = quantise_rows(x_rows, "x")
-        hidden_mx = quantise_moving(hidden_grouped, "hidden")
-        x_mx = {0: quantise_moving(x_grouped, "x")}
-
-        bias_flipped = flip_pool.tile([P, P], BF16, name="bias_flipped", tag="flip")
-        nc.tensor.transpose(bias_flipped[:], bias_rows[:], ident_bf16[:])
-        bias_both = const.tile([P, P], F32)
-        nc.vector.tensor_copy(out=bias_both[:], in_=bias_flipped[:])
         bias = const.tile([P, half_p], F32)
-        nc.vector.tensor_add(out=bias[:], in0=bias_both[:, 0:half_p], in1=bias_both[:, half_p:P])
+
+        def prepare_bias():
+            bias_flipped = flip_pool.tile([P, P], BF16, name="bias_flipped", tag="flip")
+            nc.tensor.transpose(bias_flipped[:], bias_rows[:], ident_bf16[:])
+            bias_both = const.tile([P, P], F32)
+            nc.vector.tensor_copy(out=bias_both[:], in_=bias_flipped[:])
+            nc.vector.tensor_add(out=bias[:], in0=bias_both[:, 0:half_p], in1=bias_both[:, half_p:P])
 
         cell = {}
-        for hf in range(2):
+
+        def prepare_cell(hf):
             cell_flipped = flip_pool.tile([P, TILES, B], BF16, name="cell_flipped", tag="flip")
             for jt in range(TILES):
                 for a in range(B_TILES):
@@ -145,47 +180,94 @@ def tile_lstm_pa_kernel(tc, x, hidden, cell_state, w_ih, w_hh, b_ih, b_hh, out_0
             else:
                 nc.scalar.copy(out=cell[(0, hf)][:], in_=cell_flipped[:])
 
+        units = list_units()
+        steps = [(u, q) for u in range(len(units)) for q in range(CHUNKS_PER_GATE)]
+        n_steps = len(steps)
         grouped = {}
+        mixed = {}
         z = {}
         gate_sb = {}
+        gate_of = {}
         tanh_c = {}
         flipped_out = {}
+        moving = {}
         x1_grouped = rows_pool.tile([P, PASSES, B * PACK], BF16, align_bytes=64)
 
-        def unit_of(u):
-            return u // (2 * N_GATES), (u // 2) % N_GATES, u % 2
+        def turn(n, part):
+            return int((n + 1) * part) > int(n * part)
 
-        def regroup(s):
-            u, q = s // CHUNKS_PER_GATE, s % CHUNKS_PER_GATE
-            layer, pos, hf = unit_of(u)
+        def regrouper(s):
+            if s < SHARED_HEAD or units[steps[s][0]][3] < HALF:
+                return "shared"
+            if turn(s, TENSOR_SHARE) and units[steps[s][0]][1] + units[steps[s][0]][0] > 0:
+                return "tensor"
+            return "vector" if turn(s - int(s * TENSOR_SHARE), VECTOR_SHARE) else "scalar"
+
+        def source(s):
+            u, q = steps[s]
+            layer, pos, first, width = units[u]
             c = (layer * N_GATES + pos) * CHUNKS_PER_GATE + q
-            grouped[s] = grouped_pool.tile([P, HALF, PACK], BF16, name="grouped", align_bytes=64)
-            first = hf * HALF
-            split = first + VECTOR_COLS
-            nc.vector.tensor_copy(
-                out=grouped[s][:, 0:VECTOR_COLS, :].rearrange("p (c i) t -> p c t i", i=2),
-                in_=raw[c][:, :, first:split].rearrange("p t (c i) -> p c t i", i=2),
+            at = first % HALF
+            return raw[(c, first // HALF)][:, :, at : at + width], width
+
+        def mix(s):
+            src, width = source(s)
+            mixed[s] = []
+            for first in range(0, width, MIX_COLS):
+                tile = flip_pool.tile([P, MIX_COLS, PACK], BF16, name="mixed", tag="flip")
+                for t in range(0, PACK, 2):
+                    nc.tensor.matmul(
+                        tile[:, :, t : t + 2].rearrange("p n t -> p t n"),
+                        lhsT=ident_bf16[:],
+                        rhs=src[:, t : t + 2, first : first + MIX_COLS],
+                        start=True,
+                        stop=True,
+                    )
+                mixed[s].append(tile)
+
+        def regroup(s, on_vector):
+            src, width = source(s)
+            by = regrouper(s)
+            if by == "shared":
+                split = int(width * (HEAD_SHARE if s < SHARED_HEAD else TAIL_SHARE))
+            else:
+                split = width if by == "vector" else 0
+            cols = slice(0, split) if on_vector else slice(split, width)
+            if cols.start == cols.stop:
+                return
+            if s not in grouped:
+                grouped[s] = grouped_pool.tile([P, width, PACK], BF16, name="grouped", align_bytes=64)
+            if by == "tensor":
+                for i, tile in enumerate(mixed[s]):
+                    nc.scalar.copy(out=grouped[s][:, i * MIX_COLS : (i + 1) * MIX_COLS, :], in_=tile[:])
+                return
+            copy = nc.vector.tensor_copy if on_vector else nc.scalar.copy
+            copy(
+                out=grouped[s][:, cols, :].rearrange("p (c i) t -> p c t i", i=2),
+                in_=src[:, :, cols].rearrange("p t (c i) -> p c t i", i=2),
             )
-            nc.scalar.copy(
-                out=grouped[s][:, VECTOR_COLS:HALF, :].rearrange("p (c i) t -> p c t i", i=2),
-                in_=raw[c][:, :, split : first + HALF].rearrange("p t (c i) -> p c t i", i=2),
-            )
-            if hf == 1 and c + RAW_BUFS < N_CHUNKS:
+
+        def refill(s):
+            u, q = steps[s]
+            layer, pos, first, width = units[u]
+            c = (layer * N_GATES + pos) * CHUNKS_PER_GATE + q
+            if first + width == H and CHUNKS_PER_GATE <= c and c + RAW_BUFS < N_CHUNKS:
                 load_chunk(c + RAW_BUFS)
 
         def quantise_and_multiply(s):
-            u, q = s // CHUNKS_PER_GATE, s % CHUNKS_PER_GATE
-            layer, pos, hf = unit_of(u)
-            codes = codes_pool.tile([P, HALF], U32, name="codes", align_bytes=64)
-            scales = codes_pool.tile([P, HALF], U8, name="scales", align_bytes=64)
+            u, q = steps[s]
+            layer, pos, first, width = units[u]
+            tiles = width // P
+            codes = codes_pool.tile([P, width], U32, name="codes", align_bytes=64)
+            scales = codes_pool.tile([P, width], U8, name="scales", align_bytes=64)
             nc.vector.quantize_mx(
                 out=codes[:].bitcast(FP8X4), scales=scales[:], in_=grouped[s][:].rearrange("p n t -> p (n t)")
             )
             if q == 0:
-                z[u] = [z_pool.tile([P, B], F32, name="z", tag="z") for jt in range(TILES)]
-            moving_codes, moving_scales = hidden_mx if q < PASSES else x_mx[layer]
+                z[u] = [z_pool.tile([P, B], F32, name="z", tag="z") for jt in range(tiles)]
+            moving_codes, moving_scales = moving["hidden"] if q < PASSES else moving[layer]
             g = q % PASSES
-            for jt in range(TILES):
+            for jt in range(tiles):
                 nc.tensor.matmul_mx(
                     out=z[u][jt][:],
                     lhsT=codes[:, jt * P : (jt + 1) * P].bitcast(FP8X4),
@@ -197,11 +279,12 @@ def tile_lstm_pa_kernel(tc, x, hidden, cell_state, w_ih, w_hh, b_ih, b_hh, out_0
                 )
 
         def activate(u):
-            layer, pos, hf = unit_of(u)
+            layer, pos, first, width = units[u]
             gate = GATE_ORDER[pos]
-            gate_sb[u] = gate_pool.tile([P, TILES, B], F32, name="gate%d" % gate)
-            for jt in range(TILES):
-                col = (gate * LAYERS + layer) * (H // P) + hf * TILES + jt
+            gate_sb[u] = gate_pool.tile([P, width // P, B], F32, name="gate%d" % gate)
+            gate_of[(layer, pos, first // HALF)] = gate_sb[u]
+            for jt in range(width // P):
+                col = (gate * LAYERS + layer) * (H // P) + first // P + jt
                 nc.scalar.activation(
                     out=gate_sb[u][:, jt, :],
                     in_=z[u][jt][:],
@@ -210,11 +293,11 @@ def tile_lstm_pa_kernel(tc, x, hidden, cell_state, w_ih, w_hh, b_ih, b_hh, out_0
                     scale=1.0,
                 )
 
-        def flip_sum(terms, key):
+        def flip_sum(terms, tiles, key):
             flipped_out[key] = []
             for a in range(B_TILES):
-                flipped = flip_pool.tile([P, HALF], F32, name="flipped_out", tag="flip")
-                for jt in range(TILES):
+                flipped = flip_pool.tile([P, tiles * P], F32, name="flipped_out", tag="flip")
+                for jt in range(tiles):
                     for i, term in enumerate(terms):
                         nc.tensor.matmul(
                             flipped[:, jt * P : (jt + 1) * P],
@@ -226,38 +309,42 @@ def tile_lstm_pa_kernel(tc, x, hidden, cell_state, w_ih, w_hh, b_ih, b_hh, out_0
                         )
                 flipped_out[key].append(flipped)
 
-        def store_rows(rows, out, a, hf):
-            nc.sync.dma_start(out=out[a * P : (a + 1) * P, hf * HALF : (hf + 1) * HALF], in_=rows[:])
-
         def update_cell(u):
-            layer, pos, hf = unit_of(u)
+            layer, pos, first, width = units[u]
+            hf = first // HALF
+            here = gate_sb[u]
             if pos == 1:
-                nc.vector.tensor_mul(out=gate_sb[u - 2][:], in0=gate_sb[u - 2][:], in1=gate_sb[u][:])
+                i_gate = gate_of[(layer, 0, hf)]
+                nc.vector.tensor_mul(out=i_gate[:], in0=i_gate[:], in1=here[:])
             if pos == 2:
-                nc.vector.tensor_mul(out=gate_sb[u][:], in0=gate_sb[u][:], in1=cell[(layer, hf)][:])
+                nc.vector.tensor_mul(out=here[:], in0=here[:], in1=cell[(layer, hf)][:])
+                i_times_g = gate_of[(layer, 0, hf)]
                 if layer == 0:
                     cell[(1, hf)] = cell_pool.tile([P, TILES, B], F32, name="cell")
-                    nc.vector.tensor_add(out=cell[(1, hf)][:], in0=gate_sb[u][:], in1=gate_sb[u - 4][:])
+                    nc.vector.tensor_add(out=cell[(1, hf)][:], in0=here[:], in1=i_times_g[:])
                 else:
-                    flip_sum((gate_sb[u], gate_sb[u - 4]), u)
-            if pos == 3:
-                if layer == 0:
+                    flip_sum((here, i_times_g), TILES, u)
+            if pos == 3 and layer == 0:
+                nc.vector.tensor_mul(
+                    out=x1_grouped[:, hf, :].rearrange("p (b t) -> p b t", t=PACK),
+                    in0=here[:].rearrange("p t b -> p b t"),
+                    in1=tanh_c[(0, hf)][:].rearrange("p t b -> p b t"),
+                )
+                if hf == 1:
+                    moving[1] = quantise_moving(x1_grouped, "x1")
+            if pos == 3 and layer == 1:
+                flip_sum((here,), width // P, u)
+                at = first % HALF
+                for a in range(B_TILES):
+                    rows = store_pool.tile([P, width], F32, name="out_rows")
                     nc.vector.tensor_mul(
-                        out=x1_grouped[:, hf, :].rearrange("p (b t) -> p b t", t=PACK),
-                        in0=gate_sb[u][:].rearrange("p t b -> p b t"),
-                        in1=tanh_c[(layer, hf)][:].rearrange("p t b -> p b t"),
+                        out=rows[:], in0=flipped_out[u][a][:], in1=tanh_c[(1, hf)][a][:, at : at + width]
                     )
-                    if hf == 1:
-                        x_mx[1] = quantise_moving(x1_grouped, "x1")
-                else:
-                    flip_sum((gate_sb[u],), u)
-                    for a in range(B_TILES):
-                        rows = store_pool.tile([P, HALF], F32, name="out_rows")
-                        nc.vector.tensor_mul(out=rows[:], in0=flipped_out[u][a][:], in1=tanh_c[(1, hf)][a][:])
-                        store_rows(rows, out_0, a, hf)
+                    nc.sync.dma_start(out=out_0[a * P : (a + 1) * P, first : first + width], in_=rows[:])
 
         def after_cell(u):
-            layer, pos, hf = unit_of(u)
+            layer, pos, first, width = units[u]
+            hf = first // HALF
             if pos == 2 and layer == 0:
                 tanh_c[(0, hf)] = gate_pool.tile([P, TILES, B], F32, name="tanh_c")
                 nc.scalar.activation(out=tanh_c[(0, hf)][:], in_=cell[(1, hf)][:], func=TANH)
@@ -265,21 +352,42 @@ def tile_lstm_pa_kernel(tc, x, hidden, cell_state, w_ih, w_hh, b_ih, b_hh, out_0
                 tanh_c[(1, hf)] = []
                 for a in range(B_TILES):
                     rows = store_pool.tile([P, HALF], F32, name="out_rows")
-                    nc.scalar.copy(out=rows[:], in_=flipped_out[u][a][:])
-                    store_rows(rows, out_1, a, hf)
+                    (nc.vector.tensor_copy if a < C2_ON_VECTOR else nc.scalar.copy)(out=rows[:], in_=flipped_out[u][a][:])
+                    nc.sync.dma_start(out=out_1[a * P : (a + 1) * P, first : first + width], in_=rows[:])
                     tanh_rows = tanh_pool.tile([P, HALF], F32, name="tanh_rows")
                     nc.scalar.activation(out=tanh_rows[:], in_=flipped_out[u][a][:], func=TANH)
                     tanh_c[(1, hf)].append(tanh_rows)
 
         last = CHUNKS_PER_GATE - 1
-        for s in range(N_STEPS + 7):
-            if s < N_STEPS:
-                regroup(s)
-            if 2 <= s < N_STEPS + 2 and (s - 2) % CHUNKS_PER_GATE == last:
-                activate((s - 2) // CHUNKS_PER_GATE)
-            if 4 <= s < N_STEPS + 4 and (s - 4) % CHUNKS_PER_GATE == last:
-                update_cell((s - 4) // CHUNKS_PER_GATE)
-            if 6 <= s < N_STEPS + 6 and (s - 6) % CHUNKS_PER_GATE == last:
-                after_cell((s - 6) // CHUNKS_PER_GATE)
-            if 1 <= s <= N_STEPS:
-                quantise_and_multiply(s - 1)
+
+        def unit_ending(s):
+            return steps[s][0] if 0 <= s < n_steps and steps[s][1] == last else None
+
+        scalar_steps = {}
+        for s in range(n_steps):
+            at = s if s < SHARED_HEAD else max(SHARED_HEAD, s - SCALAR_LEAD)
+            scalar_steps.setdefault(at, []).append(s)
+
+        for s in range(n_steps + QUANT_LAG + TANH_LAG + 1):
+            if s + TENSOR_LEAD < n_steps and regrouper(s + TENSOR_LEAD) == "tensor":
+                mix(s + TENSOR_LEAD)
+            if s < n_steps:
+                regroup(s, on_vector=True)
+            for ahead in scalar_steps.get(s, []):
+                regroup(ahead, on_vector=False)
+            if s < n_steps:
+                refill(s)
+            if s == 1:
+                moving["hidden"] = quantise_rows(hidden_rows, "hidden")
+            if s == 2:
+                moving[0] = quantise_rows(x_rows, "x")
+            if s == 4:
+                prepare_bias()
+            if s in (12, 13):
+                prepare_cell(s - 12)
+            for lag, act in ((ACT_LAG, activate), (CELL_LAG, update_cell), (TANH_LAG, after_cell)):
+                u = unit_ending(s - QUANT_LAG - lag)
+                if u is not None:
+                    act(u)
+            if 0 <= s - QUANT_LAG < n_steps:
+                quantise_and_multiply(s - QUANT_LAG)

@@ -26,24 +26,24 @@ GATE_ORDER = (0, 2, 1, 3)
 N_GATES = len(GATE_ORDER)
 CHUNKS_PER_GATE = 2 * PASSES
 N_CHUNKS = LAYERS * N_GATES * CHUNKS_PER_GATE
-RAW_BUFS = 6
-TENSOR_SHARE = 1 / 5
-VECTOR_SHARE = 5 / 8
+RAW_BUFS = 8
+TENSOR_COLS = 112
+VECTOR_COLS = 224
+HEAD_COLS = 272
+LAST_COLS = 272
+TAIL_COLS = 224
 TENSOR_LEAD = 4
 SCALAR_LEAD = 3
-QUANT_LAG = 1
-HEAD_SHARE = 17 / 32
-TAIL_SHARE = 7 / 8
+QUANT_LAG = 2
 C2_ON_VECTOR = 0
 SHARED_HEAD = 4
+CELL_STEPS = (12, 15)
+LATE_LAST = 1
 ACT_LAG = 1
 CELL_LAG = 3
 TANH_LAG = 5
 CODES_BUFS = 6
-Z_BUFS = 6
 
-
-MIX_COLS = 256
 
 FLOPS = 2 * LAYERS * N_GATES * 2 * B * H * H
 
@@ -59,7 +59,7 @@ def tile_lstm_pa_kernel(tc, x, hidden, cell_state, w_ih, w_hh, b_ih, b_hh, out_0
     with ExitStack() as ctx:
         const = ctx.enter_context(tc.tile_pool(name="const", bufs=1))
         rows_pool = ctx.enter_context(tc.tile_pool(name="rows", bufs=1))
-        raw_half_pool = ctx.enter_context(tc.tile_pool(name="raw_half", bufs=2 * CHUNKS_PER_GATE))
+        raw_half_pool = ctx.enter_context(tc.tile_pool(name="raw_half", bufs=2))
         raw_pool = ctx.enter_context(tc.tile_pool(name="raw", bufs=RAW_BUFS))
         grouped_pool = ctx.enter_context(tc.tile_pool(name="grouped", bufs=SCALAR_LEAD + QUANT_LAG + 2))
         codes_pool = ctx.enter_context(tc.tile_pool(name="codes", bufs=CODES_BUFS))
@@ -67,8 +67,7 @@ def tile_lstm_pa_kernel(tc, x, hidden, cell_state, w_ih, w_hh, b_ih, b_hh, out_0
         cell_pool = ctx.enter_context(tc.tile_pool(name="cell", bufs=2))
         tanh_pool = ctx.enter_context(tc.tile_pool(name="tanh", bufs=2 * B_TILES))
         store_pool = ctx.enter_context(tc.tile_pool(name="store", bufs=8))
-        z_pool = ctx.enter_context(tc.psum_pool(name="z", bufs=Z_BUFS))
-        flip_pool = ctx.enter_context(tc.psum_pool(name="flip", bufs=8 - Z_BUFS))
+        bank_pool = ctx.enter_context(tc.psum_pool(name="bank", bufs=8))
 
         def load_rows(src, name):
             rows = rows_pool.tile([P, B_TILES, H], BF16, name=name)
@@ -104,15 +103,12 @@ def tile_lstm_pa_kernel(tc, x, hidden, cell_state, w_ih, w_hh, b_ih, b_hh, out_0
 
         load_half(0, 0)
         hidden_rows = load_rows(hidden, "hidden_rows")
-        load_half(1, 0)
+        load_half(0, 1)
         x_rows = load_rows(x, "x_rows")
-        load_half(2, 0)
-        load_half(3, 0)
-        for c in range(CHUNKS_PER_GATE):
-            load_half(c, 1)
-        load_chunk(CHUNKS_PER_GATE)
+        for c in range(1, CHUNKS_PER_GATE + 1):
+            load_chunk(c)
         cell_rows = load_rows(cell_state, "cell_rows")
-        for c in range(CHUNKS_PER_GATE + 1, CHUNKS_PER_GATE + RAW_BUFS):
+        for c in range(CHUNKS_PER_GATE + 1, 1 + RAW_BUFS):
             load_chunk(c)
 
         ident_f32 = const.tile([P, P], F32)
@@ -133,55 +129,60 @@ def tile_lstm_pa_kernel(tc, x, hidden, cell_state, w_ih, w_hh, b_ih, b_hh, out_0
             )
             return codes, scales
 
-        def quantise_rows(rows, name):
+        def flip_rows(rows):
             words = rows[:].bitcast(F32)
-            grouped = rows_pool.tile([P, PASSES, B * PACK], BF16, name=name + "_grouped", align_bytes=64)
-            grouped_words = grouped[:].bitcast(F32)
+            flipped = []
             for g in range(PASSES):
-                flipped = flip_pool.tile([P, 2, B], F32, name="flipped", tag="flip")
+                tile = bank_pool.tile([P, 2, B], F32, name="flipped", tag="bank")
                 for u in range(2):
                     for a in range(B_TILES):
                         first = g * (K_PASS // 2) + u
                         nc.tensor.transpose(
-                            flipped[:, u, a * P : (a + 1) * P],
+                            tile[:, u, a * P : (a + 1) * P],
                             words[:, a, first : (g + 1) * (K_PASS // 2) : 2],
                             ident_f32[:],
                         )
-                dst = grouped_words[:, g, :].rearrange("p (b u) -> p b u", u=2)
-                src = flipped[:].rearrange("p u b -> p b u")
-                if g == 0:
-                    nc.vector.tensor_copy(out=dst, in_=src)
-                else:
-                    nc.scalar.copy(out=dst, in_=src)
-            return quantise_moving(grouped, name)
+                flipped.append(tile)
+            return flipped
 
+        def group_rows(flipped, name, copy):
+            grouped = rows_pool.tile([P, PASSES, B * PACK], BF16, name=name + "_grouped", align_bytes=64)
+            grouped_words = grouped[:].bitcast(F32)
+            for g in range(PASSES):
+                dst = grouped_words[:, g, :].rearrange("p (b u) -> p b u", u=2)
+                copy(out=dst, in_=flipped[g][:].rearrange("p u b -> p b u"))
+            return grouped
+
+        bias_both = const.tile([P, P], F32)
         bias = const.tile([P, half_p], F32)
 
-        def prepare_bias():
-            bias_flipped = flip_pool.tile([P, P], BF16, name="bias_flipped", tag="flip")
+        def flip_bias():
+            bias_flipped = bank_pool.tile([P, P], BF16, name="bias_flipped", tag="bank")
             nc.tensor.transpose(bias_flipped[:], bias_rows[:], ident_bf16[:])
-            bias_both = const.tile([P, P], F32)
-            nc.vector.tensor_copy(out=bias_both[:], in_=bias_flipped[:])
+            nc.scalar.copy(out=bias_both[:], in_=bias_flipped[:])
+
+        def add_bias():
             nc.vector.tensor_add(out=bias[:], in0=bias_both[:, 0:half_p], in1=bias_both[:, half_p:P])
 
         cell = {}
 
-        def prepare_cell(hf):
-            cell_flipped = flip_pool.tile([P, TILES, B], BF16, name="cell_flipped", tag="flip")
+        def flip_cell(hf):
+            cell_flipped = bank_pool.tile([P, TILES, B], BF16, name="cell_flipped", tag="bank")
             for jt in range(TILES):
                 for a in range(B_TILES):
                     first = hf * HALF + jt * P
                     nc.tensor.transpose(
                         cell_flipped[:, jt, a * P : (a + 1) * P], cell_rows[:, a, first : first + P], ident_bf16[:]
                     )
+            return cell_flipped
+
+        def keep_cell(hf, cell_flipped):
             cell[(0, hf)] = const.tile([P, TILES, B], BF16, name="cell_0_%d" % hf)
-            if hf == 0:
-                nc.vector.tensor_copy(out=cell[(0, hf)][:], in_=cell_flipped[:])
-            else:
-                nc.scalar.copy(out=cell[(0, hf)][:], in_=cell_flipped[:])
+            nc.scalar.copy(out=cell[(0, hf)][:], in_=cell_flipped[:])
 
         units = list_units()
-        steps = [(u, q) for u in range(len(units)) for q in range(CHUNKS_PER_GATE)]
+        steps = [(u, q) for q in range(CHUNKS_PER_GATE) for u in range(2)]
+        steps += [(u, q) for u in range(2, len(units)) for q in range(CHUNKS_PER_GATE)]
         n_steps = len(steps)
         grouped = {}
         mixed = {}
@@ -193,65 +194,59 @@ def tile_lstm_pa_kernel(tc, x, hidden, cell_state, w_ih, w_hh, b_ih, b_hh, out_0
         moving = {}
         x1_grouped = rows_pool.tile([P, PASSES, B * PACK], BF16, align_bytes=64)
 
-        def turn(n, part):
-            return int((n + 1) * part) > int(n * part)
-
-        def regrouper(s):
-            if s < SHARED_HEAD or units[steps[s][0]][3] < HALF:
-                return "shared"
-            if turn(s, TENSOR_SHARE) and units[steps[s][0]][1] + units[steps[s][0]][0] > 0:
-                return "tensor"
-            return "vector" if turn(s - int(s * TENSOR_SHARE), VECTOR_SHARE) else "scalar"
+        def shares(s):
+            layer, pos, first, width = units[steps[s][0]]
+            if layer == 0 and pos < 2:
+                tensor, vector = 0, HEAD_COLS
+            elif width < HALF:
+                tensor, vector = 0, TAIL_COLS
+            elif layer == LAYERS - 1 and pos == N_GATES - 1:
+                tensor, vector = TENSOR_COLS, LAST_COLS
+            else:
+                tensor, vector = TENSOR_COLS, VECTOR_COLS
+            return tensor, vector, width - tensor - vector
 
         def source(s):
             u, q = steps[s]
             layer, pos, first, width = units[u]
             c = (layer * N_GATES + pos) * CHUNKS_PER_GATE + q
             at = first % HALF
-            return raw[(c, first // HALF)][:, :, at : at + width], width
+            return raw[(c, first // HALF)][:, :, at : at + width]
 
         def mix(s):
-            src, width = source(s)
-            mixed[s] = []
-            for first in range(0, width, MIX_COLS):
-                tile = flip_pool.tile([P, MIX_COLS, PACK], BF16, name="mixed", tag="flip")
-                for t in range(0, PACK, 2):
-                    nc.tensor.matmul(
-                        tile[:, :, t : t + 2].rearrange("p n t -> p t n"),
-                        lhsT=ident_bf16[:],
-                        rhs=src[:, t : t + 2, first : first + MIX_COLS],
-                        start=True,
-                        stop=True,
-                    )
-                mixed[s].append(tile)
+            tensor = shares(s)[0]
+            mixed[s] = bank_pool.tile([P, TENSOR_COLS, PACK], BF16, name="mixed", tag="bank")
+            nc.tensor.matmul(
+                mixed[s][:].rearrange("p n t -> p t n"),
+                lhsT=ident_bf16[:],
+                rhs=source(s)[:, :, 0:tensor],
+                start=True,
+                stop=True,
+            )
 
         def regroup(s, on_vector):
-            src, width = source(s)
-            by = regrouper(s)
-            if by == "shared":
-                split = int(width * (HEAD_SHARE if s < SHARED_HEAD else TAIL_SHARE))
-            else:
-                split = width if by == "vector" else 0
-            cols = slice(0, split) if on_vector else slice(split, width)
-            if cols.start == cols.stop:
-                return
+            tensor, vector, scalar = shares(s)
+            width = tensor + vector + scalar
             if s not in grouped:
                 grouped[s] = grouped_pool.tile([P, width, PACK], BF16, name="grouped", align_bytes=64)
-            if by == "tensor":
-                for i, tile in enumerate(mixed[s]):
-                    nc.scalar.copy(out=grouped[s][:, i * MIX_COLS : (i + 1) * MIX_COLS, :], in_=tile[:])
-                return
-            copy = nc.vector.tensor_copy if on_vector else nc.scalar.copy
-            copy(
-                out=grouped[s][:, cols, :].rearrange("p (c i) t -> p c t i", i=2),
-                in_=src[:, :, cols].rearrange("p t (c i) -> p c t i", i=2),
-            )
+            cols = slice(tensor, tensor + vector) if on_vector else slice(tensor + vector, width)
+            if not on_vector and tensor:
+                nc.scalar.copy(
+                    out=grouped[s][:, 0:tensor, :].rearrange("p n t -> p (n t)").bitcast(F32),
+                    in_=mixed[s][:].rearrange("p n t -> p (n t)").bitcast(F32),
+                )
+            if cols.start < cols.stop:
+                copy = nc.vector.tensor_copy if on_vector else nc.scalar.copy
+                copy(
+                    out=grouped[s][:, cols, :].rearrange("p (c i) t -> p c t i", i=4),
+                    in_=source(s)[:, :, cols].rearrange("p t (c i) -> p c t i", i=4),
+                )
 
         def refill(s):
             u, q = steps[s]
             layer, pos, first, width = units[u]
             c = (layer * N_GATES + pos) * CHUNKS_PER_GATE + q
-            if first + width == H and CHUNKS_PER_GATE <= c and c + RAW_BUFS < N_CHUNKS:
+            if first + width == H and 1 <= c and c + RAW_BUFS < N_CHUNKS:
                 load_chunk(c + RAW_BUFS)
 
         def quantise_and_multiply(s):
@@ -264,7 +259,7 @@ def tile_lstm_pa_kernel(tc, x, hidden, cell_state, w_ih, w_hh, b_ih, b_hh, out_0
                 out=codes[:].bitcast(FP8X4), scales=scales[:], in_=grouped[s][:].rearrange("p n t -> p (n t)")
             )
             if q == 0:
-                z[u] = [z_pool.tile([P, B], F32, name="z", tag="z") for jt in range(tiles)]
+                z[u] = [bank_pool.tile([P, B], F32, name="z", tag="bank") for jt in range(tiles)]
             moving_codes, moving_scales = moving["hidden"] if q < PASSES else moving[layer]
             g = q % PASSES
             for jt in range(tiles):
@@ -296,7 +291,7 @@ def tile_lstm_pa_kernel(tc, x, hidden, cell_state, w_ih, w_hh, b_ih, b_hh, out_0
         def flip_sum(terms, tiles, key):
             flipped_out[key] = []
             for a in range(B_TILES):
-                flipped = flip_pool.tile([P, tiles * P], F32, name="flipped_out", tag="flip")
+                flipped = bank_pool.tile([P, tiles * P], F32, name="flipped_out", tag="bank")
                 for jt in range(tiles):
                     for i, term in enumerate(terms):
                         nc.tensor.matmul(
@@ -360,16 +355,26 @@ def tile_lstm_pa_kernel(tc, x, hidden, cell_state, w_ih, w_hh, b_ih, b_hh, out_0
 
         last = CHUNKS_PER_GATE - 1
 
-        def unit_ending(s):
-            return steps[s][0] if 0 <= s < n_steps and steps[s][1] == last else None
+        after = {}
+        for s in range(n_steps):
+            u, q = steps[s]
+            if q == last:
+                layer, pos, first, width = units[u]
+                end = s + QUANT_LAG
+                in_last_gate = layer == LAYERS - 1 and pos == N_GATES - 1
+                after.setdefault(end + ACT_LAG, []).append((u, activate))
+                update = max(end + CELL_LAG, n_steps + QUANT_LAG) if in_last_gate and LATE_LAST else end + CELL_LAG
+                after.setdefault(update, []).append((u, update_cell))
+                after.setdefault(end + TANH_LAG, []).append((u, after_cell))
 
+        cell_flipped = {}
         scalar_steps = {}
         for s in range(n_steps):
             at = s if s < SHARED_HEAD else max(SHARED_HEAD, s - SCALAR_LEAD)
             scalar_steps.setdefault(at, []).append(s)
 
         for s in range(n_steps + QUANT_LAG + TANH_LAG + 1):
-            if s + TENSOR_LEAD < n_steps and regrouper(s + TENSOR_LEAD) == "tensor":
+            if s + TENSOR_LEAD < n_steps and shares(s + TENSOR_LEAD)[0] > 0:
                 mix(s + TENSOR_LEAD)
             if s < n_steps:
                 regroup(s, on_vector=True)
@@ -377,17 +382,23 @@ def tile_lstm_pa_kernel(tc, x, hidden, cell_state, w_ih, w_hh, b_ih, b_hh, out_0
                 regroup(ahead, on_vector=False)
             if s < n_steps:
                 refill(s)
+            if s == 0:
+                hidden_flipped = flip_rows(hidden_rows)
             if s == 1:
-                moving["hidden"] = quantise_rows(hidden_rows, "hidden")
+                hidden_grouped = group_rows(hidden_flipped, "hidden", nc.vector.tensor_copy)
+                moving["hidden"] = quantise_moving(hidden_grouped, "hidden")
+                x_flipped = flip_rows(x_rows)
             if s == 2:
-                moving[0] = quantise_rows(x_rows, "x")
-            if s == 4:
-                prepare_bias()
-            if s in (12, 13):
-                prepare_cell(s - 12)
-            for lag, act in ((ACT_LAG, activate), (CELL_LAG, update_cell), (TANH_LAG, after_cell)):
-                u = unit_ending(s - QUANT_LAG - lag)
-                if u is not None:
-                    act(u)
+                x_grouped = group_rows(x_flipped, "x", nc.scalar.copy)
+                flip_bias()
+            if s == 3:
+                moving[0] = quantise_moving(x_grouped, "x")
+                add_bias()
+            if s in CELL_STEPS:
+                cell_flipped[s] = flip_cell(CELL_STEPS.index(s))
+            if s - 2 in CELL_STEPS:
+                keep_cell(CELL_STEPS.index(s - 2), cell_flipped[s - 2])
+            for at, act in after.get(s, []):
+                act(at)
             if 0 <= s - QUANT_LAG < n_steps:
                 quantise_and_multiply(s - QUANT_LAG)

@@ -27,17 +27,16 @@ N_GATES = len(GATE_ORDER)
 CHUNKS_PER_GATE = 2 * PASSES
 N_CHUNKS = LAYERS * N_GATES * CHUNKS_PER_GATE
 RAW_BUFS = 8
-TENSOR_COLS = 112
-VECTOR_COLS = 224
-HEAD_COLS = 272
-LAST_COLS = 272
+TENSOR_COLS = 128
+VECTOR_COLS = 216
+HEAD_COLS = 264
+LAST_COLS = 256
 TAIL_COLS = 224
 TENSOR_LEAD = 4
 SCALAR_LEAD = 3
 QUANT_LAG = 2
 C2_ON_VECTOR = 0
 SHARED_HEAD = 4
-CELL_STEPS = (12, 15)
 LATE_LAST = 1
 ACT_LAG = 1
 CELL_LAG = 3
@@ -174,11 +173,7 @@ def tile_lstm_pa_kernel(tc, x, hidden, cell_state, w_ih, w_hh, b_ih, b_hh, out_0
                     nc.tensor.transpose(
                         cell_flipped[:, jt, a * P : (a + 1) * P], cell_rows[:, a, first : first + P], ident_bf16[:]
                     )
-            return cell_flipped
-
-        def keep_cell(hf, cell_flipped):
-            cell[(0, hf)] = const.tile([P, TILES, B], BF16, name="cell_0_%d" % hf)
-            nc.scalar.copy(out=cell[(0, hf)][:], in_=cell_flipped[:])
+            cell[(0, hf)] = cell_flipped
 
         units = list_units()
         steps = [(u, q) for q in range(CHUNKS_PER_GATE) for u in range(2)]
@@ -278,6 +273,8 @@ def tile_lstm_pa_kernel(tc, x, hidden, cell_state, w_ih, w_hh, b_ih, b_hh, out_0
             gate = GATE_ORDER[pos]
             gate_sb[u] = gate_pool.tile([P, width // P, B], F32, name="gate%d" % gate)
             gate_of[(layer, pos, first // HALF)] = gate_sb[u]
+            if layer == 0 and pos == 2:
+                flip_cell(first // HALF)
             for jt in range(width // P):
                 col = (gate * LAYERS + layer) * (H // P) + first // P + jt
                 nc.scalar.activation(
@@ -367,7 +364,6 @@ def tile_lstm_pa_kernel(tc, x, hidden, cell_state, w_ih, w_hh, b_ih, b_hh, out_0
                 after.setdefault(update, []).append((u, update_cell))
                 after.setdefault(end + TANH_LAG, []).append((u, after_cell))
 
-        cell_flipped = {}
         scalar_steps = {}
         for s in range(n_steps):
             at = s if s < SHARED_HEAD else max(SHARED_HEAD, s - SCALAR_LEAD)
@@ -394,10 +390,6 @@ def tile_lstm_pa_kernel(tc, x, hidden, cell_state, w_ih, w_hh, b_ih, b_hh, out_0
             if s == 3:
                 moving[0] = quantise_moving(x_grouped, "x")
                 add_bias()
-            if s in CELL_STEPS:
-                cell_flipped[s] = flip_cell(CELL_STEPS.index(s))
-            if s - 2 in CELL_STEPS:
-                keep_cell(CELL_STEPS.index(s - 2), cell_flipped[s - 2])
             for at, act in after.get(s, []):
                 act(at)
             if 0 <= s - QUANT_LAG < n_steps:

@@ -26,31 +26,36 @@ GATE_ORDER = (0, 2, 1, 3)
 N_GATES = len(GATE_ORDER)
 CHUNKS_PER_GATE = 2 * PASSES
 N_CHUNKS = LAYERS * N_GATES * CHUNKS_PER_GATE
-RAW_BUFS = 8
+RAW_BUFS = 6
 TENSOR_COLS = 128
 VECTOR_COLS = 216
-HEAD_COLS = 264
-LAST_COLS = 256
+HEAD_COLS = 280
+LAST_COLS = 272
 TAIL_COLS = 224
-TENSOR_LEAD = 4
-SCALAR_LEAD = 3
-QUANT_LAG = 2
+TENSOR_LEAD = 2
+SCALAR_LEAD = 1
+QUANT_LAG = 1
 C2_ON_VECTOR = 0
 SHARED_HEAD = 4
-LATE_LAST = 1
+GATE_BUFS = 2
 ACT_LAG = 1
-CELL_LAG = 3
-TANH_LAG = 5
-CODES_BUFS = 6
+CELL_LAG = 1
+TANH_LAG = 0
+CODES_BUFS = 7
 
 
 FLOPS = 2 * LAYERS * N_GATES * 2 * B * H * H
 
 
-def list_units():
-    units = [(layer, pos, hf * HALF, HALF) for layer in range(LAYERS) for pos in range(N_GATES) for hf in range(2)]
+def list_blocks():
+    last = (LAYERS - 1, N_GATES - 1)
+    gates = [(layer, pos) for layer in range(LAYERS) for pos in range(N_GATES)]
     quarter = HALF // 2
-    return units[:-1] + [(LAYERS - 1, N_GATES - 1, HALF + i * quarter, quarter) for i in range(2)]
+    return [g + (0, H) for g in gates if g != last] + [
+        last + (0, HALF),
+        last + (HALF, quarter),
+        last + (HALF + quarter, quarter),
+    ]
 
 
 def tile_lstm_pa_kernel(tc, x, hidden, cell_state, w_ih, w_hh, b_ih, b_hh, out_0, out_1):
@@ -62,7 +67,7 @@ def tile_lstm_pa_kernel(tc, x, hidden, cell_state, w_ih, w_hh, b_ih, b_hh, out_0
         raw_pool = ctx.enter_context(tc.tile_pool(name="raw", bufs=RAW_BUFS))
         grouped_pool = ctx.enter_context(tc.tile_pool(name="grouped", bufs=SCALAR_LEAD + QUANT_LAG + 2))
         codes_pool = ctx.enter_context(tc.tile_pool(name="codes", bufs=CODES_BUFS))
-        gate_pool = ctx.enter_context(tc.tile_pool(name="gate", bufs=2))
+        gate_pool = ctx.enter_context(tc.tile_pool(name="gate", bufs=GATE_BUFS))
         cell_pool = ctx.enter_context(tc.tile_pool(name="cell", bufs=2))
         tanh_pool = ctx.enter_context(tc.tile_pool(name="tanh", bufs=2 * B_TILES))
         store_pool = ctx.enter_context(tc.tile_pool(name="store", bufs=8))
@@ -87,13 +92,12 @@ def tile_lstm_pa_kernel(tc, x, hidden, cell_state, w_ih, w_hh, b_ih, b_hh, out_0
         def load_half(c, hf):
             tile = raw_half_pool.tile([P, PACK, HALF], BF16, name="raw_half")
             nc.sync.dma_start(out=tile[:], in_=chunk_view(c)[:, :, hf * HALF : (hf + 1) * HALF])
-            raw[(c, hf)] = tile[:]
+            raw[(c, hf)] = tile
 
         def load_chunk(c):
             tile = raw_pool.tile([P, PACK, H], BF16, name="raw")
             nc.sync.dma_start(out=tile[:], in_=chunk_view(c))
-            for hf in range(2):
-                raw[(c, hf)] = tile[:, :, hf * HALF : (hf + 1) * HALF]
+            raw[c] = tile
 
         half_p = P // 2
         bias_rows = const.tile([P, P], BF16)
@@ -175,115 +179,125 @@ def tile_lstm_pa_kernel(tc, x, hidden, cell_state, w_ih, w_hh, b_ih, b_hh, out_0
                     )
             cell[(0, hf)] = cell_flipped
 
-        units = list_units()
-        steps = [(u, q) for q in range(CHUNKS_PER_GATE) for u in range(2)]
-        steps += [(u, q) for u in range(2, len(units)) for q in range(CHUNKS_PER_GATE)]
+        blocks = list_blocks()
+        steps = [(b, q) for b in range(len(blocks)) for q in range(CHUNKS_PER_GATE)]
         n_steps = len(steps)
         grouped = {}
         mixed = {}
+        codes_of = {}
         z = {}
-        gate_sb = {}
         gate_of = {}
         tanh_c = {}
         flipped_out = {}
         moving = {}
         x1_grouped = rows_pool.tile([P, PASSES, B * PACK], BF16, align_bytes=64)
 
-        def shares(s):
-            layer, pos, first, width = units[steps[s][0]]
-            if layer == 0 and pos < 2:
-                tensor, vector = 0, HEAD_COLS
-            elif width < HALF:
-                tensor, vector = 0, TAIL_COLS
-            elif layer == LAYERS - 1 and pos == N_GATES - 1:
-                tensor, vector = TENSOR_COLS, LAST_COLS
-            else:
-                tensor, vector = TENSOR_COLS, VECTOR_COLS
-            return tensor, vector, width - tensor - vector
+        def chunk_of(s):
+            b, q = steps[s]
+            layer, pos, first, width = blocks[b]
+            return (layer * N_GATES + pos) * CHUNKS_PER_GATE + q
 
-        def source(s):
-            u, q = steps[s]
-            layer, pos, first, width = units[u]
-            c = (layer * N_GATES + pos) * CHUNKS_PER_GATE + q
-            at = first % HALF
-            return raw[(c, first // HALF)][:, :, at : at + width]
+        def pieces(s):
+            b, q = steps[s]
+            layer, pos, first, width = blocks[b]
+            c = chunk_of(s)
+            if c == 0:
+                return [(raw[(0, hf)], 0, HEAD_COLS, HALF - HEAD_COLS) for hf in range(2)]
+            src = raw[c][:, :, first : first + width]
+            if layer == 0 and pos < 2:
+                return [(src, 0, 2 * HEAD_COLS, H - 2 * HEAD_COLS)]
+            if width == H:
+                return [(src, 2 * TENSOR_COLS, 2 * VECTOR_COLS, H - 2 * TENSOR_COLS - 2 * VECTOR_COLS)]
+            if width == HALF:
+                return [(src, TENSOR_COLS, LAST_COLS, HALF - TENSOR_COLS - LAST_COLS)]
+            return [(src, 0, TAIL_COLS, width - TAIL_COLS)]
 
         def mix(s):
-            tensor = shares(s)[0]
-            mixed[s] = bank_pool.tile([P, TENSOR_COLS, PACK], BF16, name="mixed", tag="bank")
-            nc.tensor.matmul(
-                mixed[s][:].rearrange("p n t -> p t n"),
-                lhsT=ident_bf16[:],
-                rhs=source(s)[:, :, 0:tensor],
-                start=True,
-                stop=True,
-            )
+            src, tensor, vector, scalar = pieces(s)[0]
+            mixed[s] = []
+            for first in range(0, tensor, TENSOR_COLS):
+                tile = bank_pool.tile([P, TENSOR_COLS, PACK], BF16, name="mixed", tag="bank")
+                nc.tensor.matmul(
+                    tile[:].rearrange("p n t -> p t n"),
+                    lhsT=ident_bf16[:],
+                    rhs=src[:, :, first : first + TENSOR_COLS],
+                    start=True,
+                    stop=True,
+                )
+                mixed[s].append(tile)
 
         def regroup(s, on_vector):
-            tensor, vector, scalar = shares(s)
-            width = tensor + vector + scalar
+            width = blocks[steps[s][0]][3]
             if s not in grouped:
                 grouped[s] = grouped_pool.tile([P, width, PACK], BF16, name="grouped", align_bytes=64)
-            cols = slice(tensor, tensor + vector) if on_vector else slice(tensor + vector, width)
-            if not on_vector and tensor:
-                nc.scalar.copy(
-                    out=grouped[s][:, 0:tensor, :].rearrange("p n t -> p (n t)").bitcast(F32),
-                    in_=mixed[s][:].rearrange("p n t -> p (n t)").bitcast(F32),
-                )
-            if cols.start < cols.stop:
+            at = 0
+            for src, tensor, vector, scalar in pieces(s):
+                if not on_vector:
+                    for i in range(tensor // TENSOR_COLS):
+                        cols = slice(i * TENSOR_COLS, (i + 1) * TENSOR_COLS)
+                        nc.scalar.copy(
+                            out=grouped[s][:, cols, :].rearrange("p n t -> p (n t)").bitcast(F32),
+                            in_=mixed[s][i][:].rearrange("p n t -> p (n t)").bitcast(F32),
+                        )
+                first, count = (tensor, vector) if on_vector else (tensor + vector, scalar)
                 copy = nc.vector.tensor_copy if on_vector else nc.scalar.copy
                 copy(
-                    out=grouped[s][:, cols, :].rearrange("p (c i) t -> p c t i", i=4),
-                    in_=source(s)[:, :, cols].rearrange("p t (c i) -> p c t i", i=4),
+                    out=grouped[s][:, at + first : at + first + count, :].rearrange("p (c i) t -> p c t i", i=4),
+                    in_=src[:, :, first : first + count].rearrange("p t (c i) -> p c t i", i=4),
                 )
+                at += tensor + vector + scalar
 
         def refill(s):
-            u, q = steps[s]
-            layer, pos, first, width = units[u]
-            c = (layer * N_GATES + pos) * CHUNKS_PER_GATE + q
+            layer, pos, first, width = blocks[steps[s][0]]
+            c = chunk_of(s)
             if first + width == H and 1 <= c and c + RAW_BUFS < N_CHUNKS:
                 load_chunk(c + RAW_BUFS)
 
-        def quantise_and_multiply(s):
-            u, q = steps[s]
-            layer, pos, first, width = units[u]
-            tiles = width // P
+        def quantise(s):
+            b, q = steps[s]
+            width = blocks[b][3]
             codes = codes_pool.tile([P, width], U32, name="codes", align_bytes=64)
             scales = codes_pool.tile([P, width], U8, name="scales", align_bytes=64)
             nc.vector.quantize_mx(
                 out=codes[:].bitcast(FP8X4), scales=scales[:], in_=grouped[s][:].rearrange("p n t -> p (n t)")
             )
+            codes_of[(b, q)] = codes, scales
+
+        def multiply(b, q, jt):
+            layer, pos, first, width = blocks[b]
+            codes, scales = codes_of[(b, q)]
             if q == 0:
-                z[u] = [bank_pool.tile([P, B], F32, name="z", tag="bank") for jt in range(tiles)]
+                z[(b, jt)] = bank_pool.tile([P, B], F32, name="z", tag="bank")
             moving_codes, moving_scales = moving["hidden"] if q < PASSES else moving[layer]
             g = q % PASSES
-            for jt in range(tiles):
-                nc.tensor.matmul_mx(
-                    out=z[u][jt][:],
-                    lhsT=codes[:, jt * P : (jt + 1) * P].bitcast(FP8X4),
-                    lhsT_scale=scales[:, jt * P : (jt + 1) * P],
-                    rhs=moving_codes[:, g, :].bitcast(FP8X4),
-                    rhs_scale=moving_scales[:, g, :],
-                    start=(q == 0),
-                    stop=(q == CHUNKS_PER_GATE - 1),
-                )
+            nc.tensor.matmul_mx(
+                out=z[(b, jt)][:],
+                lhsT=codes[:, jt * P : (jt + 1) * P].bitcast(FP8X4),
+                lhsT_scale=scales[:, jt * P : (jt + 1) * P],
+                rhs=moving_codes[:, g, :].bitcast(FP8X4),
+                rhs_scale=moving_scales[:, g, :],
+                start=(q == 0),
+                stop=(q == CHUNKS_PER_GATE - 1),
+            )
 
-        def activate(u):
-            layer, pos, first, width = units[u]
+        def activate(b, tiles):
+            layer, pos, first, width = blocks[b]
             gate = GATE_ORDER[pos]
-            gate_sb[u] = gate_pool.tile([P, width // P, B], F32, name="gate%d" % gate)
-            gate_of[(layer, pos, first // HALF)] = gate_sb[u]
-            if layer == 0 and pos == 2:
-                flip_cell(first // HALF)
-            for jt in range(width // P):
+            half = (first + tiles[0] * P) // HALF
+            here = gate_pool.tile([P, len(tiles), B], F32, name="gate%d" % gate)
+            for i, jt in enumerate(tiles):
                 col = (gate * LAYERS + layer) * (H // P) + first // P + jt
                 nc.scalar.activation(
-                    out=gate_sb[u][:, jt, :],
-                    in_=z[u][jt][:],
+                    out=here[:, i, :],
+                    in_=z[(b, jt)][:],
                     func=(TANH if gate == 2 else SIGMOID),
                     bias=bias[:, col : col + 1],
                     scale=1.0,
                 )
+            gate_of[(layer, pos, half)] = here
+            if layer == 0 and pos == 2:
+                flip_cell(half)
+            return here
 
         def flip_sum(terms, tiles, key):
             flipped_out[key] = []
@@ -301,10 +315,10 @@ def tile_lstm_pa_kernel(tc, x, hidden, cell_state, w_ih, w_hh, b_ih, b_hh, out_0
                         )
                 flipped_out[key].append(flipped)
 
-        def update_cell(u):
-            layer, pos, first, width = units[u]
+        def update_cell(layer, pos, first, here):
             hf = first // HALF
-            here = gate_sb[u]
+            width = here.shape[1] * P
+            key = (layer, pos, first)
             if pos == 1:
                 i_gate = gate_of[(layer, 0, hf)]
                 nc.vector.tensor_mul(out=i_gate[:], in0=i_gate[:], in1=here[:])
@@ -315,7 +329,7 @@ def tile_lstm_pa_kernel(tc, x, hidden, cell_state, w_ih, w_hh, b_ih, b_hh, out_0
                     cell[(1, hf)] = cell_pool.tile([P, TILES, B], F32, name="cell")
                     nc.vector.tensor_add(out=cell[(1, hf)][:], in0=here[:], in1=i_times_g[:])
                 else:
-                    flip_sum((here, i_times_g), TILES, u)
+                    flip_sum((here, i_times_g), TILES, key)
             if pos == 3 and layer == 0:
                 nc.vector.tensor_mul(
                     out=x1_grouped[:, hf, :].rearrange("p (b t) -> p b t", t=PACK),
@@ -325,18 +339,18 @@ def tile_lstm_pa_kernel(tc, x, hidden, cell_state, w_ih, w_hh, b_ih, b_hh, out_0
                 if hf == 1:
                     moving[1] = quantise_moving(x1_grouped, "x1")
             if pos == 3 and layer == 1:
-                flip_sum((here,), width // P, u)
+                flip_sum((here,), width // P, key)
                 at = first % HALF
                 for a in range(B_TILES):
                     rows = store_pool.tile([P, width], F32, name="out_rows")
                     nc.vector.tensor_mul(
-                        out=rows[:], in0=flipped_out[u][a][:], in1=tanh_c[(1, hf)][a][:, at : at + width]
+                        out=rows[:], in0=flipped_out[key][a][:], in1=tanh_c[(1, hf)][a][:, at : at + width]
                     )
                     nc.sync.dma_start(out=out_0[a * P : (a + 1) * P, first : first + width], in_=rows[:])
 
-        def after_cell(u):
-            layer, pos, first, width = units[u]
+        def after_cell(layer, pos, first):
             hf = first // HALF
+            key = (layer, pos, first)
             if pos == 2 and layer == 0:
                 tanh_c[(0, hf)] = gate_pool.tile([P, TILES, B], F32, name="tanh_c")
                 nc.scalar.activation(out=tanh_c[(0, hf)][:], in_=cell[(1, hf)][:], func=TANH)
@@ -344,53 +358,63 @@ def tile_lstm_pa_kernel(tc, x, hidden, cell_state, w_ih, w_hh, b_ih, b_hh, out_0
                 tanh_c[(1, hf)] = []
                 for a in range(B_TILES):
                     rows = store_pool.tile([P, HALF], F32, name="out_rows")
-                    (nc.vector.tensor_copy if a < C2_ON_VECTOR else nc.scalar.copy)(out=rows[:], in_=flipped_out[u][a][:])
-                    nc.sync.dma_start(out=out_1[a * P : (a + 1) * P, first : first + width], in_=rows[:])
+                    (nc.vector.tensor_copy if a < C2_ON_VECTOR else nc.scalar.copy)(out=rows[:], in_=flipped_out[key][a][:])
+                    nc.sync.dma_start(out=out_1[a * P : (a + 1) * P, first : first + HALF], in_=rows[:])
                     tanh_rows = tanh_pool.tile([P, HALF], F32, name="tanh_rows")
-                    nc.scalar.activation(out=tanh_rows[:], in_=flipped_out[u][a][:], func=TANH)
+                    nc.scalar.activation(out=tanh_rows[:], in_=flipped_out[key][a][:], func=TANH)
                     tanh_c[(1, hf)].append(tanh_rows)
 
-        last = CHUNKS_PER_GATE - 1
+        def mix_ahead(s):
+            if s < n_steps and pieces(s)[0][1] > 0:
+                mix(s)
 
-        after = {}
-        for s in range(n_steps):
-            u, q = steps[s]
-            if q == last:
-                layer, pos, first, width = units[u]
-                end = s + QUANT_LAG
-                in_last_gate = layer == LAYERS - 1 and pos == N_GATES - 1
-                after.setdefault(end + ACT_LAG, []).append((u, activate))
-                update = max(end + CELL_LAG, n_steps + QUANT_LAG) if in_last_gate and LATE_LAST else end + CELL_LAG
-                after.setdefault(update, []).append((u, update_cell))
-                after.setdefault(end + TANH_LAG, []).append((u, after_cell))
+        pending = {}
+        def later(s, act):
+            pending.setdefault(s, []).append(act)
 
-        scalar_steps = {}
-        for s in range(n_steps):
-            at = s if s < SHARED_HEAD else max(SHARED_HEAD, s - SCALAR_LEAD)
-            scalar_steps.setdefault(at, []).append(s)
-
-        for s in range(n_steps + QUANT_LAG + TANH_LAG + 1):
-            if s + TENSOR_LEAD < n_steps and shares(s + TENSOR_LEAD)[0] > 0:
-                mix(s + TENSOR_LEAD)
+        for s in range(n_steps + 8):
+            mix_ahead(s + TENSOR_LEAD)
             if s < n_steps:
                 regroup(s, on_vector=True)
-            for ahead in scalar_steps.get(s, []):
-                regroup(ahead, on_vector=False)
+            if s == 0:
+                for ahead in range(SCALAR_LEAD):
+                    regroup(ahead, on_vector=False)
+            if s + SCALAR_LEAD < n_steps:
+                regroup(s + SCALAR_LEAD, on_vector=False)
             if s < n_steps:
                 refill(s)
             if s == 0:
                 hidden_flipped = flip_rows(hidden_rows)
-            if s == 1:
                 hidden_grouped = group_rows(hidden_flipped, "hidden", nc.vector.tensor_copy)
                 moving["hidden"] = quantise_moving(hidden_grouped, "hidden")
                 x_flipped = flip_rows(x_rows)
-            if s == 2:
                 x_grouped = group_rows(x_flipped, "x", nc.scalar.copy)
                 flip_bias()
-            if s == 3:
+            if s == 1:
                 moving[0] = quantise_moving(x_grouped, "x")
                 add_bias()
-            for at, act in after.get(s, []):
-                act(at)
-            if 0 <= s - QUANT_LAG < n_steps:
-                quantise_and_multiply(s - QUANT_LAG)
+            for act in pending.get(s, []):
+                act()
+            if not 0 <= s - QUANT_LAG < n_steps:
+                continue
+            quantise(s - QUANT_LAG)
+            b, q = steps[s - QUANT_LAG]
+            layer, pos, first, width = blocks[b]
+            front = range(min(width // P, TILES))
+            for jt in front:
+                multiply(b, q, jt)
+            if q < CHUNKS_PER_GATE - 1:
+                continue
+            halves = [(front, first)]
+            if width == H:
+                halves.append((range(TILES, 2 * TILES), HALF))
+                for jt in halves[1][0]:
+                    for p in range(CHUNKS_PER_GATE):
+                        multiply(b, p, jt)
+
+            for i, (tiles, at) in enumerate(halves):
+                def work(b=b, layer=layer, pos=pos, tiles=tiles, at=at, s=s):
+                    here = activate(b, tiles)
+                    later(s + ACT_LAG + CELL_LAG, lambda: update_cell(layer, pos, at, here))
+                    later(s + ACT_LAG + CELL_LAG + TANH_LAG, lambda: after_cell(layer, pos, at))
+                later(s + ACT_LAG, work)

from contextlib import ExitStack

import concourse.mybir as mybir
from concourse.masks import make_identity

BF16 = mybir.dt.bfloat16
F32 = mybir.dt.float32
U32 = mybir.dt.uint32
U8 = mybir.dt.uint8
FP8X4 = mybir.dt.float8_e4m3fn_x4
SIGMOID = mybir.ActivationFunctionType.Sigmoid
TANH = mybir.ActivationFunctionType.Tanh

P = 128
PACK = 4
K_PASS = P * PACK
B = 256
H = 1024
LAYERS = 2
PASSES = H // K_PASS
HALF = H // 2
TILES = HALF // P
B_TILES = B // P

GATE_ORDER = (0, 2, 1, 3)
N_GATES = len(GATE_ORDER)
CHUNKS_PER_GATE = 2 * PASSES
N_CHUNKS = LAYERS * N_GATES * CHUNKS_PER_GATE
RAW_BUFS = 6
TENSOR_COLS = 128
VECTOR_COLS = 216
HEAD_COLS = 280
LAST_COLS = 272
TAIL_COLS = 224
TENSOR_LEAD = 2
SCALAR_LEAD = 1
QUANT_LAG = 1
C2_ON_VECTOR = 0
SHARED_HEAD = 4
GATE_BUFS = 2
ACT_LAG = 1
CELL_LAG = 1
TANH_LAG = 0
CODES_BUFS = 7


FLOPS = 2 * LAYERS * N_GATES * 2 * B * H * H


def list_blocks():
    last = (LAYERS - 1, N_GATES - 1)
    gates = [(layer, pos) for layer in range(LAYERS) for pos in range(N_GATES)]
    quarter = HALF // 2
    return [g + (0, H) for g in gates if g != last] + [
        last + (0, HALF),
        last + (HALF, quarter),
        last + (HALF + quarter, quarter),
    ]


def tile_lstm_pa_kernel(tc, x, hidden, cell_state, w_ih, w_hh, b_ih, b_hh, out_0, out_1):
    nc = tc.nc
    with ExitStack() as ctx:
        const = ctx.enter_context(tc.tile_pool(name="const", bufs=1))
        rows_pool = ctx.enter_context(tc.tile_pool(name="rows", bufs=1))
        raw_half_pool = ctx.enter_context(tc.tile_pool(name="raw_half", bufs=2))
        raw_pool = ctx.enter_context(tc.tile_pool(name="raw", bufs=RAW_BUFS))
        grouped_pool = ctx.enter_context(tc.tile_pool(name="grouped", bufs=SCALAR_LEAD + QUANT_LAG + 2))
        codes_pool = ctx.enter_context(tc.tile_pool(name="codes", bufs=CODES_BUFS))
        gate_pool = ctx.enter_context(tc.tile_pool(name="gate", bufs=GATE_BUFS))
        cell_pool = ctx.enter_context(tc.tile_pool(name="cell", bufs=2))
        tanh_pool = ctx.enter_context(tc.tile_pool(name="tanh", bufs=2 * B_TILES))
        store_pool = ctx.enter_context(tc.tile_pool(name="store", bufs=8))
        bank_pool = ctx.enter_context(tc.psum_pool(name="bank", bufs=8))

        def load_rows(src, name):
            rows = rows_pool.tile([P, B_TILES, H], BF16, name=name)
            nc.sync.dma_start(out=rows[:], in_=src.rearrange("(a p) k -> p a k", p=P))
            return rows

        raw = {}

        def chunk_view(c):
            layer, pos, q = c // (N_GATES * CHUNKS_PER_GATE), (c // CHUNKS_PER_GATE) % N_GATES, c % CHUNKS_PER_GATE
            w = w_hh if q < PASSES else w_ih
            g = q % PASSES
            k_rows = w[GATE_ORDER[pos], layer, g * K_PASS : (g + 1) * K_PASS, :]
            if layer == 1 and q >= PASSES:
                return k_rows.rearrange("(t p) n -> p t n", p=P)
            return k_rows.rearrange("(p t) n -> p t n", t=PACK)

        def load_half(c, hf):
            tile = raw_half_pool.tile([P, PACK, HALF], BF16, name="raw_half")
            nc.sync.dma_start(out=tile[:], in_=chunk_view(c)[:, :, hf * HALF : (hf + 1) * HALF])
            raw[(c, hf)] = tile

        def load_chunk(c):
            tile = raw_pool.tile([P, PACK, H], BF16, name="raw")
            nc.sync.dma_start(out=tile[:], in_=chunk_view(c))
            raw[c] = tile

        half_p = P // 2
        bias_rows = const.tile([P, P], BF16)
        nc.scalar.dma_start(out=bias_rows[0:half_p, :], in_=b_ih.rearrange("k l (j p) -> (k l j) p", p=P))
        nc.scalar.dma_start(out=bias_rows[half_p:P, :], in_=b_hh.rearrange("k l (j p) -> (k l j) p", p=P))

        load_half(0, 0)
        hidden_rows = load_rows(hidden, "hidden_rows")
        load_half(0, 1)
        x_rows = load_rows(x, "x_rows")
        for c in range(1, CHUNKS_PER_GATE + 1):
            load_chunk(c)
        cell_rows = load_rows(cell_state, "cell_rows")
        for c in range(CHUNKS_PER_GATE + 1, 1 + RAW_BUFS):
            load_chunk(c)

        ident_f32 = const.tile([P, P], F32)
        make_identity(nc, ident_f32[:])
        ident_bf16 = const.tile([P, P], BF16)
        make_identity(nc, ident_bf16[:])
        warm = const.tile([P, 1], F32)
        nc.vector.memset(warm[:], 0.0)
        nc.scalar.activation(out=warm[:], in_=warm[:], func=SIGMOID)

        def quantise_moving(grouped, name):
            codes = const.tile([P, PASSES, B], U32, name=name + "_codes", align_bytes=64)
            scales = const.tile([P, PASSES, B], U8, name=name + "_scales", align_bytes=64)
            nc.vector.quantize_mx(
                out=codes[:].rearrange("p g b -> p (g b)").bitcast(FP8X4),
                scales=scales[:].rearrange("p g b -> p (g b)"),
                in_=grouped[:].rearrange("p g c -> p (g c)"),
            )
            return codes, scales

        def flip_rows(rows):
            words = rows[:].bitcast(F32)
            flipped = []
            for g in range(PASSES):
                tile = bank_pool.tile([P, 2, B], F32, name="flipped", tag="bank")
                for u in range(2):
                    for a in range(B_TILES):
                        first = g * (K_PASS // 2) + u
                        nc.tensor.transpose(
                            tile[:, u, a * P : (a + 1) * P],
                            words[:, a, first : (g + 1) * (K_PASS // 2) : 2],
                            ident_f32[:],
                        )
                flipped.append(tile)
            return flipped

        def group_rows(flipped, name, copy):
            grouped = rows_pool.tile([P, PASSES, B * PACK], BF16, name=name + "_grouped", align_bytes=64)
            grouped_words = grouped[:].bitcast(F32)
            for g in range(PASSES):
                dst = grouped_words[:, g, :].rearrange("p (b u) -> p b u", u=2)
                copy(out=dst, in_=flipped[g][:].rearrange("p u b -> p b u"))
            return grouped

        bias_both = const.tile([P, P], F32)
        bias = const.tile([P, half_p], F32)

        def flip_bias():
            bias_flipped = bank_pool.tile([P, P], BF16, name="bias_flipped", tag="bank")
            nc.tensor.transpose(bias_flipped[:], bias_rows[:], ident_bf16[:])
            nc.scalar.copy(out=bias_both[:], in_=bias_flipped[:])

        def add_bias():
            nc.vector.tensor_add(out=bias[:], in0=bias_both[:, 0:half_p], in1=bias_both[:, half_p:P])

        cell = {}

        def flip_cell(hf):
            cell_flipped = bank_pool.tile([P, TILES, B], BF16, name="cell_flipped", tag="bank")
            for jt in range(TILES):
                for a in range(B_TILES):
                    first = hf * HALF + jt * P
                    nc.tensor.transpose(
                        cell_flipped[:, jt, a * P : (a + 1) * P], cell_rows[:, a, first : first + P], ident_bf16[:]
                    )
            cell[(0, hf)] = cell_flipped

        blocks = list_blocks()
        steps = [(b, q) for b in range(len(blocks)) for q in range(CHUNKS_PER_GATE)]
        n_steps = len(steps)
        grouped = {}
        mixed = {}
        codes_of = {}
        z = {}
        gate_of = {}
        tanh_c = {}
        flipped_out = {}
        moving = {}
        x1_grouped = rows_pool.tile([P, PASSES, B * PACK], BF16, align_bytes=64)

        def chunk_of(s):
            b, q = steps[s]
            layer, pos, first, width = blocks[b]
            return (layer * N_GATES + pos) * CHUNKS_PER_GATE + q

        def pieces(s):
            b, q = steps[s]
            layer, pos, first, width = blocks[b]
            c = chunk_of(s)
            if c == 0:
                return [(raw[(0, hf)], 0, HEAD_COLS, HALF - HEAD_COLS) for hf in range(2)]
            src = raw[c][:, :, first : first + width]
            if layer == 0 and pos < 2:
                return [(src, 0, 2 * HEAD_COLS, H - 2 * HEAD_COLS)]
            if width == H:
                return [(src, 2 * TENSOR_COLS, 2 * VECTOR_COLS, H - 2 * TENSOR_COLS - 2 * VECTOR_COLS)]
            if width == HALF:
                return [(src, TENSOR_COLS, LAST_COLS, HALF - TENSOR_COLS - LAST_COLS)]
            return [(src, 0, TAIL_COLS, width - TAIL_COLS)]

        def mix(s):
            src, tensor, vector, scalar = pieces(s)[0]
            mixed[s] = []
            for first in range(0, tensor, TENSOR_COLS):
                tile = bank_pool.tile([P, TENSOR_COLS, PACK], BF16, name="mixed", tag="bank")
                nc.tensor.matmul(
                    tile[:].rearrange("p n t -> p t n"),
                    lhsT=ident_bf16[:],
                    rhs=src[:, :, first : first + TENSOR_COLS],
                    start=True,
                    stop=True,
                )
                mixed[s].append(tile)

        def regroup(s, on_vector):
            width = blocks[steps[s][0]][3]
            if s not in grouped:
                grouped[s] = grouped_pool.tile([P, width, PACK], BF16, name="grouped", align_bytes=64)
            at = 0
            for src, tensor, vector, scalar in pieces(s):
                if not on_vector:
                    for i in range(tensor // TENSOR_COLS):
                        cols = slice(i * TENSOR_COLS, (i + 1) * TENSOR_COLS)
                        nc.scalar.copy(
                            out=grouped[s][:, cols, :].rearrange("p n t -> p (n t)").bitcast(F32),
                            in_=mixed[s][i][:].rearrange("p n t -> p (n t)").bitcast(F32),
                        )
                first, count = (tensor, vector) if on_vector else (tensor + vector, scalar)
                copy = nc.vector.tensor_copy if on_vector else nc.scalar.copy
                copy(
                    out=grouped[s][:, at + first : at + first + count, :].rearrange("p (c i) t -> p c t i", i=4),
                    in_=src[:, :, first : first + count].rearrange("p t (c i) -> p c t i", i=4),
                )
                at += tensor + vector + scalar

        def refill(s):
            layer, pos, first, width = blocks[steps[s][0]]
            c = chunk_of(s)
            if first + width == H and 1 <= c and c + RAW_BUFS < N_CHUNKS:
                load_chunk(c + RAW_BUFS)

        def quantise(s):
            b, q = steps[s]
            width = blocks[b][3]
            codes = codes_pool.tile([P, width], U32, name="codes", align_bytes=64)
            scales = codes_pool.tile([P, width], U8, name="scales", align_bytes=64)
            nc.vector.quantize_mx(
                out=codes[:].bitcast(FP8X4), scales=scales[:], in_=grouped[s][:].rearrange("p n t -> p (n t)")
            )
            codes_of[(b, q)] = codes, scales

        def multiply(b, q, jt):
            layer, pos, first, width = blocks[b]
            codes, scales = codes_of[(b, q)]
            if q == 0:
                z[(b, jt)] = bank_pool.tile([P, B], F32, name="z", tag="bank")
            moving_codes, moving_scales = moving["hidden"] if q < PASSES else moving[layer]
            g = q % PASSES
            nc.tensor.matmul_mx(
                out=z[(b, jt)][:],
                lhsT=codes[:, jt * P : (jt + 1) * P].bitcast(FP8X4),
                lhsT_scale=scales[:, jt * P : (jt + 1) * P],
                rhs=moving_codes[:, g, :].bitcast(FP8X4),
                rhs_scale=moving_scales[:, g, :],
                start=(q == 0),
                stop=(q == CHUNKS_PER_GATE - 1),
            )

        def activate(b, tiles):
            layer, pos, first, width = blocks[b]
            gate = GATE_ORDER[pos]
            half = (first + tiles[0] * P) // HALF
            here = gate_pool.tile([P, len(tiles), B], F32, name="gate%d" % gate)
            for i, jt in enumerate(tiles):
                col = (gate * LAYERS + layer) * (H // P) + first // P + jt
                nc.scalar.activation(
                    out=here[:, i, :],
                    in_=z[(b, jt)][:],
                    func=(TANH if gate == 2 else SIGMOID),
                    bias=bias[:, col : col + 1],
                    scale=1.0,
                )
            gate_of[(layer, pos, half)] = here
            if layer == 0 and pos == 2:
                flip_cell(half)
            return here

        def flip_sum(terms, tiles, key):
            flipped_out[key] = []
            for a in range(B_TILES):
                flipped = bank_pool.tile([P, tiles * P], F32, name="flipped_out", tag="bank")
                for jt in range(tiles):
                    for i, term in enumerate(terms):
                        nc.tensor.matmul(
                            flipped[:, jt * P : (jt + 1) * P],
                            lhsT=term[:, jt, a * P : (a + 1) * P],
                            rhs=ident_f32[:],
                            is_transpose=True,
                            start=(i == 0),
                            stop=(i == len(terms) - 1),
                        )
                flipped_out[key].append(flipped)

        def update_cell(layer, pos, first, here):
            hf = first // HALF
            width = here.shape[1] * P
            key = (layer, pos, first)
            if pos == 1:
                i_gate = gate_of[(layer, 0, hf)]
                nc.vector.tensor_mul(out=i_gate[:], in0=i_gate[:], in1=here[:])
            if pos == 2:
                nc.vector.tensor_mul(out=here[:], in0=here[:], in1=cell[(layer, hf)][:])
                i_times_g = gate_of[(layer, 0, hf)]
                if layer == 0:
                    cell[(1, hf)] = cell_pool.tile([P, TILES, B], F32, name="cell")
                    nc.vector.tensor_add(out=cell[(1, hf)][:], in0=here[:], in1=i_times_g[:])
                else:
                    flip_sum((here, i_times_g), TILES, key)
            if pos == 3 and layer == 0:
                nc.vector.tensor_mul(
                    out=x1_grouped[:, hf, :].rearrange("p (b t) -> p b t", t=PACK),
                    in0=here[:].rearrange("p t b -> p b t"),
                    in1=tanh_c[(0, hf)][:].rearrange("p t b -> p b t"),
                )
                if hf == 1:
                    moving[1] = quantise_moving(x1_grouped, "x1")
            if pos == 3 and layer == 1:
                flip_sum((here,), width // P, key)
                at = first % HALF
                for a in range(B_TILES):
                    rows = store_pool.tile([P, width], F32, name="out_rows")
                    nc.vector.tensor_mul(
                        out=rows[:], in0=flipped_out[key][a][:], in1=tanh_c[(1, hf)][a][:, at : at + width]
                    )
                    nc.sync.dma_start(out=out_0[a * P : (a + 1) * P, first : first + width], in_=rows[:])

        def after_cell(layer, pos, first):
            hf = first // HALF
            key = (layer, pos, first)
            if pos == 2 and layer == 0:
                tanh_c[(0, hf)] = gate_pool.tile([P, TILES, B], F32, name="tanh_c")
                nc.scalar.activation(out=tanh_c[(0, hf)][:], in_=cell[(1, hf)][:], func=TANH)
            if pos == 2 and layer == 1:
                tanh_c[(1, hf)] = []
                for a in range(B_TILES):
                    rows = store_pool.tile([P, HALF], F32, name="out_rows")
                    (nc.vector.tensor_copy if a < C2_ON_VECTOR else nc.scalar.copy)(out=rows[:], in_=flipped_out[key][a][:])
                    nc.sync.dma_start(out=out_1[a * P : (a + 1) * P, first : first + HALF], in_=rows[:])
                    tanh_rows = tanh_pool.tile([P, HALF], F32, name="tanh_rows")
                    nc.scalar.activation(out=tanh_rows[:], in_=flipped_out[key][a][:], func=TANH)
                    tanh_c[(1, hf)].append(tanh_rows)

        def mix_ahead(s):
            if s < n_steps and pieces(s)[0][1] > 0:
                mix(s)

        pending = {}
        def later(s, act):
            pending.setdefault(s, []).append(act)

        for s in range(n_steps + 8):
            mix_ahead(s + TENSOR_LEAD)
            if s < n_steps:
                regroup(s, on_vector=True)
            if s == 0:
                for ahead in range(SCALAR_LEAD):
                    regroup(ahead, on_vector=False)
            if s + SCALAR_LEAD < n_steps:
                regroup(s + SCALAR_LEAD, on_vector=False)
            if s < n_steps:
                refill(s)
            if s == 0:
                hidden_flipped = flip_rows(hidden_rows)
                hidden_grouped = group_rows(hidden_flipped, "hidden", nc.vector.tensor_copy)
                moving["hidden"] = quantise_moving(hidden_grouped, "hidden")
                x_flipped = flip_rows(x_rows)
                x_grouped = group_rows(x_flipped, "x", nc.scalar.copy)
                flip_bias()
            if s == 1:
                moving[0] = quantise_moving(x_grouped, "x")
                add_bias()
            for act in pending.get(s, []):
                act()
            if not 0 <= s - QUANT_LAG < n_steps:
                continue
            quantise(s - QUANT_LAG)
            b, q = steps[s - QUANT_LAG]
            layer, pos, first, width = blocks[b]
            front = range(min(width // P, TILES))
            for jt in front:
                multiply(b, q, jt)
            if q < CHUNKS_PER_GATE - 1:
                continue
            halves = [(front, first)]
            if width == H:
                halves.append((range(TILES, 2 * TILES), HALF))
                for jt in halves[1][0]:
                    for p in range(CHUNKS_PER_GATE):
                        multiply(b, p, jt)

            for i, (tiles, at) in enumerate(halves):
                def work(b=b, layer=layer, pos=pos, tiles=tiles, at=at, s=s):
                    here = activate(b, tiles)
                    later(s + ACT_LAG + CELL_LAG, lambda: update_cell(layer, pos, at, here))
                    later(s + ACT_LAG + CELL_LAG + TANH_LAG, lambda: after_cell(layer, pos, at))
                later(s + ACT_LAG, work)
